import numpy as np
import ml_dtypes


def mxq(x, axis, fmt="e4m3"):
    dtype, down = {"e4m3": (ml_dtypes.float8_e4m3fn, 7), "e5m2": (ml_dtypes.float8_e5m2, 14)}[fmt]
    v = np.moveaxis(np.asarray(x, np.float32).astype(ml_dtypes.bfloat16).astype(np.float64), axis, -1)
    blocks = v.reshape(v.shape[:-1] + (-1, 32))
    amax = np.abs(blocks).max(-1, keepdims=True)
    byte = np.maximum(np.where(amax > 0, np.frexp(amax)[1] - 1 + 127, 0) - down, 1)
    scale = np.exp2(byte - 127.0)
    codes = (blocks / scale).astype(np.float32).astype(dtype).astype(np.float64)
    return np.moveaxis((codes * scale).reshape(v.shape), -1, axis)


WIDE = False


def mx_kscale(k):
    if not WIDE:
        return np.ones(k)
    levels = np.array([10, -10, 5, -5, 0])
    a = np.random.permutation(np.resize(levels, k // 512 * 4)).reshape(k // 512, 4)
    idx = np.arange(k)
    return np.exp2(a[idx // 512, idx % 128 // 32])


BF16 = ml_dtypes.bfloat16


def bf(x):
    return np.asarray(x, np.float32).astype(BF16)


def f64(x):
    return np.asarray(x).astype(np.float64)


B, N, HD, ED, F = 1, 32, 128, 256, 384
TD = HD + HD
MD = TD + ED
EPS = 1e-5


def layer_norm(x, g, b):
    mu = x.mean(-1, keepdims=True)
    var = x.var(-1, keepdims=True)
    return (x - mu) * (1.0 / np.sqrt(var + EPS)) * g + b


def setup_inputs():
    s = mx_kscale(MD)
    sx, se = s[:HD], s[TD:]
    sr = np.concatenate([sx, sx, se])
    return {"p": bf(np.random.standard_normal((B, N, N, ED)) + 0.5 * np.random.standard_normal((B, N, N))[..., None]),
            "x_down": bf(np.random.standard_normal((B, N, HD)) * sx),
            "ln_edge_g": bf((1.0 + 0.1 * np.random.standard_normal(ED)) * se),
            "ln_edge_b": bf(0.1 * np.random.standard_normal(ED) * se),
            "W1": bf(np.random.standard_normal((MD, F)) / np.sqrt(MD) / sr[:, None]),
            "b1": bf(0.1 * np.random.standard_normal(F))}


def reference(p, x_down, ln_edge_g, ln_edge_b, W1, b1):
    p_ln = layer_norm(f64(p), f64(ln_edge_g), f64(ln_edge_b))
    xd = f64(x_down)
    edge_bias = np.concatenate([np.broadcast_to(xd[:, :, None, :], (B, N, N, HD)),
                                np.broadcast_to(xd[:, None, :, :], (B, N, N, HD))], axis=-1)
    z_in = np.concatenate([edge_bias, p_ln], axis=-1)
    return np.maximum((mxq(z_in, 3, "e4m3") @ mxq(f64(W1), 0, "e4m3")) + f64(b1), 0.0)

@@ -1,0 +1,177 @@
+from contextlib import ExitStack
+
+import concourse.mybir as mybir
+from concourse.masks import make_identity
+
+F32 = mybir.dt.float32
+BF16 = mybir.dt.bfloat16
+U32 = mybir.dt.uint32
+U8 = mybir.dt.uint8
+FP8X4 = mybir.dt.float8_e4m3fn_x4
+ALU = mybir.AluOpType
+ACT = mybir.ActivationFunctionType
+
+P = 128
+PACK = 4
+NODES = 32
+EDGES = NODES * NODES
+ED = 256
+F_OUT = 384
+TILES = EDGES // P
+HALVES = 2
+HALF_TILES = TILES // HALVES
+HALF_EDGES = HALF_TILES * P
+HALF_NODES = NODES // HALVES
+EPS = 1e-5
+W_SLICES = ((0, 256), (256, 128))
+FLOPS = 2 * EDGES * PACK * P * F_OUT
+
+
+def tile_edgeupdaterwrapper_v01_pa_s_kernel(tc, p, x_down, ln_edge_g, ln_edge_b, W1, b1, out):
+    nc = tc.nc
+    p_rows = p.flatten_outer_dims().rearrange("(t e) f -> e t f", e=P)
+    out_rows = out.flatten_outer_dims().rearrange("(t e) n -> e t n", e=P)
+
+    with ExitStack() as ctx:
+        keep = ctx.enter_context(tc.tile_pool(name="keep", bufs=1))
+        ps_small = ctx.enter_context(tc.psum_pool(name="ps_small", bufs=1))
+        ps_t = ctx.enter_context(tc.psum_pool(name="ps_t", bufs=4))
+        ps_acc = ctx.enter_context(tc.psum_pool(name="ps_acc", bufs=3))
+
+        p_sb = keep.tile([P, TILES, ED], BF16)
+        for c in range(0, TILES, 2):
+            nc.sync.dma_start(out=p_sb[:, c : c + 2, :], in_=p_rows[:, c : c + 2, :])
+
+        small_rows = keep.tile([P, P], BF16)
+        nc.vector.memset(small_rows[:], 0.0)
+        nc.scalar.dma_start(out=small_rows[0:NODES, :], in_=x_down.flatten_outer_dims())
+        nc.scalar.dma_start(out=small_rows[32:34, :], in_=ln_edge_g.rearrange("(u f) -> u f", u=2))
+        nc.scalar.dma_start(out=small_rows[34:36, :], in_=ln_edge_b.rearrange("(u f) -> u f", u=2))
+
+        w_raw = keep.tile([P, PACK, F_OUT], BF16)
+        nc.scalar.dma_start(out=w_raw[:], in_=W1.rearrange("(s q) n -> q s n", q=P))
+
+        bias_bc = keep.tile([P, F_OUT], BF16)
+        nc.gpsimd.dma_start(out=bias_bc[:], in_=b1.partition_broadcast(P))
+
+        eps_col = keep.tile([P, 1], F32)
+        nc.vector.memset(eps_col[:], EPS)
+        warm = keep.tile([P, 1], F32)
+        nc.scalar.activation(out=warm[:], in_=eps_col[:], func=ACT.Sqrt)
+        ident_bf = keep.tile([P, P], BF16)
+        make_identity(nc, ident_bf[:])
+        ident_f32 = keep.tile([P, P], F32)
+        make_identity(nc, ident_f32[:])
+
+        small_ps = ps_small.tile([P, P], BF16)
+        nc.tensor.transpose(out=small_ps[:], in_=small_rows[:], identity=ident_bf[:])
+        gb = keep.tile([P, 4], F32)
+        nc.scalar.copy(out=gb[:], in_=small_ps[:, 32:36])
+
+        planes = keep.tile([P, PACK, EDGES], BF16)
+        for h in range(HALVES):
+            es = slice(h * HALF_EDGES, (h + 1) * HALF_EDGES)
+            nc.scalar.copy(
+                out=planes[:, 0, es].rearrange("q (i j) -> q i j", j=NODES),
+                in_=small_ps[:, h * HALF_NODES : (h + 1) * HALF_NODES].unsqueeze(2).to_broadcast([P, HALF_NODES, NODES]),
+            )
+            nc.scalar.copy(
+                out=planes[:, 1, es].rearrange("q (i j) -> q i j", j=NODES),
+                in_=small_ps[:, 0:NODES].unsqueeze(1).to_broadcast([P, HALF_NODES, NODES]),
+            )
+
+        w_grouped = keep.tile([P, F_OUT, PACK], BF16, align_bytes=64)
+        w_codes = keep.tile([P, F_OUT], U32, align_bytes=64)
+        w_scales = keep.tile([P, F_OUT], U8, align_bytes=64)
+        for n0, nw in W_SLICES:
+            nc.gpsimd.tensor_scalar(
+                out=w_grouped[:, n0 : n0 + nw, :],
+                in0=w_raw[:, :, n0 : n0 + nw].rearrange("q s n -> q n s"),
+                scalar1=1.0,
+                scalar2=0.0,
+                op0=ALU.mult,
+                op1=ALU.add,
+            )
+        for n0, nw in W_SLICES:
+            nc.vector.quantize_mx(
+                out=w_codes[:, n0 : n0 + nw].bitcast(FP8X4),
+                scales=w_scales[:, n0 : n0 + nw],
+                in_=w_grouped[:, n0 : n0 + nw, :].rearrange("q n s -> q (n s)"),
+            )
+
+        stats = keep.tile([P, TILES, 6], F32)
+        mean_var = keep.tile([P, TILES, 2], F32)
+        std = keep.tile([P, TILES], F32)
+        rstd = keep.tile([P, TILES], F32)
+        shift = keep.tile([P, TILES], F32)
+        for h in range(HALVES):
+            hs = slice(h * HALF_TILES, (h + 1) * HALF_TILES)
+            for t in range(h * HALF_TILES, (h + 1) * HALF_TILES):
+                nc.vector.bn_stats(out=stats[:, t, :], in_=p_sb[:, t, :])
+                nc.vector.bn_aggr(out=mean_var[:, t, :], in_=stats[:, t, :])
+            nc.scalar.activation(out=std[:, hs], in_=mean_var[:, hs, 1], func=ACT.Sqrt, bias=eps_col[:], scale=1.0)
+            nc.vector.reciprocal(out=rstd[:, hs], in_=std[:, hs])
+            nc.vector.scalar_tensor_tensor(
+                out=shift[:, hs], in0=mean_var[:, hs, 0], scalar=-1.0, in1=rstd[:, hs], op0=ALU.mult, op1=ALU.mult
+            )
+
+        xhat = keep.tile([P, TILES, ED], F32)
+        for h in range(HALVES):
+            es = slice(h * HALF_EDGES, (h + 1) * HALF_EDGES)
+            for t in range(h * HALF_TILES, (h + 1) * HALF_TILES):
+                if t % 2 == 0:
+                    nc.scalar.activation(
+                        out=xhat[:, t, :], in_=p_sb[:, t, :], func=ACT.Identity,
+                        scale=rstd[:, t : t + 1], bias=shift[:, t : t + 1],
+                    )
+                else:
+                    nc.gpsimd.tensor_scalar(
+                        out=xhat[:, t, :], in0=p_sb[:, t, :],
+                        scalar1=rstd[:, t : t + 1], scalar2=shift[:, t : t + 1], op0=ALU.mult, op1=ALU.add,
+                    )
+            for u in range(2):
+                xt = ps_t.tile([P, HALF_EDGES], F32)
+                for c in range(HALF_TILES):
+                    nc.tensor.transpose(
+                        out=xt[:, c * P : (c + 1) * P],
+                        in_=xhat[:, h * HALF_TILES + c, u * P : (u + 1) * P],
+                        identity=ident_f32[:],
+                    )
+                if u == 0:
+                    nc.scalar.activation(
+                        out=planes[:, 2 + u, es], in_=xt[:], func=ACT.Identity,
+                        scale=gb[:, u : u + 1], bias=gb[:, 2 + u : 3 + u],
+                    )
+                else:
+                    nc.vector.tensor_scalar(
+                        out=planes[:, 2 + u, es], in0=xt[:],
+                        scalar1=gb[:, u : u + 1], scalar2=gb[:, 2 + u : 3 + u], op0=ALU.mult, op1=ALU.add,
+                    )
+
+        grouped = keep.tile([P, TILES, P, PACK], BF16, align_bytes=64)
+        z_codes = keep.tile([P, TILES, P], U32, align_bytes=64)
+        z_scales = keep.tile([P, TILES, P], U8, align_bytes=64)
+        result = keep.tile([P, TILES, F_OUT], F32)
+        for t in range(TILES):
+            nc.vector.tensor_copy(
+                out=grouped[:, t, :, :], in_=planes[:, :, t * P : (t + 1) * P].rearrange("q s e -> q e s")
+            )
+            nc.vector.quantize_mx(
+                out=z_codes[:, t, :].bitcast(FP8X4),
+                scales=z_scales[:, t, :],
+                in_=grouped[:, t, :, :].rearrange("q e s -> q (e s)"),
+            )
+            acc = ps_acc.tile([P, 512], F32)
+            for n0, nw in W_SLICES:
+                nc.tensor.matmul_mx(
+                    out=acc[:, n0 : n0 + nw],
+                    lhsT=z_codes[:, t, :].bitcast(FP8X4),
+                    lhsT_scale=z_scales[:, t, :],
+                    rhs=w_codes[:, n0 : n0 + nw].bitcast(FP8X4),
+                    rhs_scale=w_scales[:, n0 : n0 + nw],
+                    start=True,
+                    stop=True,
+                )
+            nc.vector.tensor_tensor(out=result[:, t, :], in0=acc[:, 0:F_OUT], in1=bias_bc[:], op=ALU.add)
+            nc.scalar.activation(out=result[:, t, :], in_=result[:, t, :], func=ACT.Relu)
+            nc.sync.dma_start(out=out_rows[:, t, :], in_=result[:, t, :])

@@ -18,12 +18,12 @@ EDGES = NODES * NODES
 ED = 256
 F_OUT = 384
 TILES = EDGES // P
-HALVES = 2
-HALF_TILES = TILES // HALVES
-HALF_EDGES = HALF_TILES * P
-HALF_NODES = NODES // HALVES
+QUARTERS = 4
+Q_TILES = TILES // QUARTERS
+Q_EDGES = Q_TILES * P
+Q_NODES = NODES // QUARTERS
 EPS = 1e-5
-W_SLICES = ((0, 256), (256, 128))
+MX_SLICES = ((0, 256), (256, 128))
 FLOPS = 2 * EDGES * PACK * P * F_OUT
 
 
@@ -33,145 +33,199 @@ def tile_edgeupdaterwrapper_v01_pa_s_kernel(tc, p, x_down, ln_edge_g, ln_edge_b,
     out_rows = out.flatten_outer_dims().rearrange("(t e) n -> e t n", e=P)
 
     with ExitStack() as ctx:
+        ctx.enter_context(tc.manual_schedule())
         keep = ctx.enter_context(tc.tile_pool(name="keep", bufs=1))
         ps_small = ctx.enter_context(tc.psum_pool(name="ps_small", bufs=1))
-        ps_t = ctx.enter_context(tc.psum_pool(name="ps_t", bufs=4))
+        ps_t = ctx.enter_context(tc.psum_pool(name="ps_t", bufs=3))
         ps_acc = ctx.enter_context(tc.psum_pool(name="ps_acc", bufs=3))
 
         p_sb = keep.tile([P, TILES, ED], BF16)
-        for c in range(0, TILES, 2):
-            nc.sync.dma_start(out=p_sb[:, c : c + 2, :], in_=p_rows[:, c : c + 2, :])
-
-        small_rows = keep.tile([P, P], BF16)
-        nc.vector.memset(small_rows[:], 0.0)
-        nc.scalar.dma_start(out=small_rows[0:NODES, :], in_=x_down.flatten_outer_dims())
-        nc.scalar.dma_start(out=small_rows[32:34, :], in_=ln_edge_g.rearrange("(u f) -> u f", u=2))
-        nc.scalar.dma_start(out=small_rows[34:36, :], in_=ln_edge_b.rearrange("(u f) -> u f", u=2))
-
+        x_rows = keep.tile([P, P], BF16)
+        gb_rows = keep.tile([P, P], BF16)
         w_raw = keep.tile([P, PACK, F_OUT], BF16)
-        nc.scalar.dma_start(out=w_raw[:], in_=W1.rearrange("(s q) n -> q s n", q=P))
-
         bias_bc = keep.tile([P, F_OUT], BF16)
-        nc.gpsimd.dma_start(out=bias_bc[:], in_=b1.partition_broadcast(P))
-
         eps_col = keep.tile([P, 1], F32)
-        nc.vector.memset(eps_col[:], EPS)
         warm = keep.tile([P, 1], F32)
-        nc.scalar.activation(out=warm[:], in_=eps_col[:], func=ACT.Sqrt)
         ident_bf = keep.tile([P, P], BF16)
-        make_identity(nc, ident_bf[:])
         ident_f32 = keep.tile([P, P], F32)
-        make_identity(nc, ident_f32[:])
-
-        small_ps = ps_small.tile([P, P], BF16)
-        nc.tensor.transpose(out=small_ps[:], in_=small_rows[:], identity=ident_bf[:])
         gb = keep.tile([P, 4], F32)
-        nc.scalar.copy(out=gb[:], in_=small_ps[:, 32:36])
-
         planes = keep.tile([P, PACK, EDGES], BF16)
-        for h in range(HALVES):
-            es = slice(h * HALF_EDGES, (h + 1) * HALF_EDGES)
-            nc.scalar.copy(
-                out=planes[:, 0, es].rearrange("q (i j) -> q i j", j=NODES),
-                in_=small_ps[:, h * HALF_NODES : (h + 1) * HALF_NODES].unsqueeze(2).to_broadcast([P, HALF_NODES, NODES]),
-            )
-            nc.scalar.copy(
-                out=planes[:, 1, es].rearrange("q (i j) -> q i j", j=NODES),
-                in_=small_ps[:, 0:NODES].unsqueeze(1).to_broadcast([P, HALF_NODES, NODES]),
-            )
-
         w_grouped = keep.tile([P, F_OUT, PACK], BF16, align_bytes=64)
         w_codes = keep.tile([P, F_OUT], U32, align_bytes=64)
         w_scales = keep.tile([P, F_OUT], U8, align_bytes=64)
-        for n0, nw in W_SLICES:
-            nc.gpsimd.tensor_scalar(
-                out=w_grouped[:, n0 : n0 + nw, :],
-                in0=w_raw[:, :, n0 : n0 + nw].rearrange("q s n -> q n s"),
-                scalar1=1.0,
-                scalar2=0.0,
-                op0=ALU.mult,
-                op1=ALU.add,
+        stats = keep.tile([P, TILES, 6], F32)
+        mean_var = keep.tile([P, TILES, 2], F32)
+        std = keep.tile([P, TILES], F32)
+        rstd = keep.tile([P, TILES], F32)
+        shift = keep.tile([P, TILES], F32)
+        xhat = keep.tile([P, TILES, ED], F32)
+        grouped = keep.tile([P, EDGES, PACK], BF16, align_bytes=64)
+        z_codes = keep.tile([P, EDGES], U32, align_bytes=64)
+        z_scales = keep.tile([P, EDGES], U8, align_bytes=64)
+        result = keep.tile([P, TILES, F_OUT], F32)
+        xt_of = {}
+        acc_of = {}
+
+        def tiles_of(q):
+            return slice(q * Q_TILES, (q + 1) * Q_TILES)
+
+        def edges_of(q):
+            return slice(q * Q_EDGES, (q + 1) * Q_EDGES)
+
+        def load_p(q):
+            nc.sync.dma_start(out=p_sb[:, tiles_of(q), :], in_=p_rows[:, tiles_of(q), :])
+
+        def statistics(q):
+            for t in range(q * Q_TILES, (q + 1) * Q_TILES):
+                nc.vector.bn_stats(out=stats[:, t, :], in_=p_sb[:, t, :])
+                nc.vector.bn_aggr(out=mean_var[:, t, :], in_=stats[:, t, :])
+            nc.scalar.activation(
+                out=std[:, tiles_of(q)], in_=mean_var[:, tiles_of(q), 1], func=ACT.Sqrt, bias=eps_col[:], scale=1.0
             )
-        for n0, nw in W_SLICES:
+
+        def scale_and_shift(q):
+            nc.vector.reciprocal(out=rstd[:, tiles_of(q)], in_=std[:, tiles_of(q)])
+            nc.vector.scalar_tensor_tensor(
+                out=shift[:, tiles_of(q)], in0=mean_var[:, tiles_of(q), 0], scalar=-1.0, in1=rstd[:, tiles_of(q)],
+                op0=ALU.mult, op1=ALU.mult,
+            )
+
+        def normalise(q):
+            for t in range(q * Q_TILES, (q + 1) * Q_TILES):
+                nc.scalar.activation(
+                    out=xhat[:, t, :], in_=p_sb[:, t, :], func=ACT.Identity,
+                    scale=rstd[:, t : t + 1], bias=shift[:, t : t + 1],
+                )
+
+        def transposes(q):
+            xt = ps_t.tile([P, 2, Q_EDGES], F32, name="xt")
+            xt_of[q] = xt
+            for u in range(2):
+                for c in range(Q_TILES):
+                    nc.tensor.transpose(
+                        out=xt[:, u, c * P : (c + 1) * P],
+                        in_=xhat[:, q * Q_TILES + c, u * P : (u + 1) * P],
+                        identity=ident_f32[:],
+                    )
+
+        def gain_and_bias(q):
+            for u in range(2):
+                nc.scalar.activation(
+                    out=planes[:, 2 + u, edges_of(q)], in_=xt_of[q][:, u, :], func=ACT.Identity,
+                    scale=gb[:, u : u + 1], bias=gb[:, 2 + u : 3 + u],
+                )
+
+        def regroup_w(n0, nw):
+            nc.gpsimd.tensor_scalar(
+                out=w_grouped[:, n0 : n0 + nw, :], in0=w_raw[:, :, n0 : n0 + nw].rearrange("q s n -> q n s"),
+                scalar1=1.0, scalar2=0.0, op0=ALU.mult, op1=ALU.add,
+            )
+
+        def quantise_w(n0, nw):
             nc.vector.quantize_mx(
                 out=w_codes[:, n0 : n0 + nw].bitcast(FP8X4),
                 scales=w_scales[:, n0 : n0 + nw],
                 in_=w_grouped[:, n0 : n0 + nw, :].rearrange("q n s -> q (n s)"),
             )
 
-        stats = keep.tile([P, TILES, 6], F32)
-        mean_var = keep.tile([P, TILES, 2], F32)
-        std = keep.tile([P, TILES], F32)
-        rstd = keep.tile([P, TILES], F32)
-        shift = keep.tile([P, TILES], F32)
-        for h in range(HALVES):
-            hs = slice(h * HALF_TILES, (h + 1) * HALF_TILES)
-            for t in range(h * HALF_TILES, (h + 1) * HALF_TILES):
-                nc.vector.bn_stats(out=stats[:, t, :], in_=p_sb[:, t, :])
-                nc.vector.bn_aggr(out=mean_var[:, t, :], in_=stats[:, t, :])
-            nc.scalar.activation(out=std[:, hs], in_=mean_var[:, hs, 1], func=ACT.Sqrt, bias=eps_col[:], scale=1.0)
-            nc.vector.reciprocal(out=rstd[:, hs], in_=std[:, hs])
-            nc.vector.scalar_tensor_tensor(
-                out=shift[:, hs], in0=mean_var[:, hs, 0], scalar=-1.0, in1=rstd[:, hs], op0=ALU.mult, op1=ALU.mult
+        def node_plane(piece):
+            h, s = divmod(piece, 2)
+            es = slice(h * EDGES // 2, (h + 1) * EDGES // 2)
+            if s == 0:
+                nodes = x_ps[:, h * NODES // 2 : (h + 1) * NODES // 2].unsqueeze(2)
+            else:
+                nodes = x_ps[:, 0:NODES].unsqueeze(1)
+            nc.scalar.copy(
+                out=planes[:, s, es].rearrange("q (i j) -> q i j", j=NODES),
+                in_=nodes.to_broadcast([P, NODES // 2, NODES]),
             )
 
-        xhat = keep.tile([P, TILES, ED], F32)
-        for h in range(HALVES):
-            es = slice(h * HALF_EDGES, (h + 1) * HALF_EDGES)
-            for t in range(h * HALF_TILES, (h + 1) * HALF_TILES):
-                if t % 2 == 0:
-                    nc.scalar.activation(
-                        out=xhat[:, t, :], in_=p_sb[:, t, :], func=ACT.Identity,
-                        scale=rstd[:, t : t + 1], bias=shift[:, t : t + 1],
-                    )
-                else:
-                    nc.gpsimd.tensor_scalar(
-                        out=xhat[:, t, :], in0=p_sb[:, t, :],
-                        scalar1=rstd[:, t : t + 1], scalar2=shift[:, t : t + 1], op0=ALU.mult, op1=ALU.add,
-                    )
-            for u in range(2):
-                xt = ps_t.tile([P, HALF_EDGES], F32)
-                for c in range(HALF_TILES):
-                    nc.tensor.transpose(
-                        out=xt[:, c * P : (c + 1) * P],
-                        in_=xhat[:, h * HALF_TILES + c, u * P : (u + 1) * P],
-                        identity=ident_f32[:],
-                    )
-                if u == 0:
-                    nc.scalar.activation(
-                        out=planes[:, 2 + u, es], in_=xt[:], func=ACT.Identity,
-                        scale=gb[:, u : u + 1], bias=gb[:, 2 + u : 3 + u],
-                    )
-                else:
-                    nc.vector.tensor_scalar(
-                        out=planes[:, 2 + u, es], in0=xt[:],
-                        scalar1=gb[:, u : u + 1], scalar2=gb[:, 2 + u : 3 + u], op0=ALU.mult, op1=ALU.add,
-                    )
-
-        grouped = keep.tile([P, TILES, P, PACK], BF16, align_bytes=64)
-        z_codes = keep.tile([P, TILES, P], U32, align_bytes=64)
-        z_scales = keep.tile([P, TILES, P], U8, align_bytes=64)
-        result = keep.tile([P, TILES, F_OUT], F32)
-        for t in range(TILES):
+        def group(q):
             nc.vector.tensor_copy(
-                out=grouped[:, t, :, :], in_=planes[:, :, t * P : (t + 1) * P].rearrange("q s e -> q e s")
+                out=grouped[:, edges_of(q), :], in_=planes[:, :, edges_of(q)].rearrange("q s e -> q e s")
             )
+
+        def quantise(q):
             nc.vector.quantize_mx(
-                out=z_codes[:, t, :].bitcast(FP8X4),
-                scales=z_scales[:, t, :],
-                in_=grouped[:, t, :, :].rearrange("q e s -> q (e s)"),
+                out=z_codes[:, edges_of(q)].bitcast(FP8X4),
+                scales=z_scales[:, edges_of(q)],
+                in_=grouped[:, edges_of(q), :].rearrange("q e s -> q (e s)"),
             )
-            acc = ps_acc.tile([P, 512], F32)
-            for n0, nw in W_SLICES:
+
+        def multiply(t):
+            acc = ps_acc.tile([P, 512], F32, name="acc")
+            acc_of[t] = acc
+            es = slice(t * P, (t + 1) * P)
+            for n0, nw in MX_SLICES:
                 nc.tensor.matmul_mx(
                     out=acc[:, n0 : n0 + nw],
-                    lhsT=z_codes[:, t, :].bitcast(FP8X4),
-                    lhsT_scale=z_scales[:, t, :],
+                    lhsT=z_codes[:, es].bitcast(FP8X4),
+                    lhsT_scale=z_scales[:, es],
                     rhs=w_codes[:, n0 : n0 + nw].bitcast(FP8X4),
                     rhs_scale=w_scales[:, n0 : n0 + nw],
                     start=True,
                     stop=True,
                 )
-            nc.vector.tensor_tensor(out=result[:, t, :], in0=acc[:, 0:F_OUT], in1=bias_bc[:], op=ALU.add)
+
+        def add_bias(t):
+            nc.vector.tensor_tensor(out=result[:, t, :], in0=acc_of[t][:, 0:F_OUT], in1=bias_bc[:], op=ALU.add)
+
+        def relu_and_store(t):
             nc.scalar.activation(out=result[:, t, :], in_=result[:, t, :], func=ACT.Relu)
             nc.sync.dma_start(out=out_rows[:, t, :], in_=result[:, t, :])
+
+        nc.sync.dma_start(out=x_rows[0:NODES, :], in_=x_down.flatten_outer_dims())
+        load_p(0)
+        load_p(1)
+        nc.sync.dma_start(out=w_raw[:], in_=W1.rearrange("(s q) n -> q s n", q=P))
+        load_p(2)
+        load_p(3)
+        nc.gpsimd.memset(gb_rows[:], 0.0)
+        nc.scalar.dma_start(out=gb_rows[0:2, :], in_=ln_edge_g.rearrange("(u f) -> u f", u=2))
+        nc.scalar.dma_start(out=gb_rows[2:4, :], in_=ln_edge_b.rearrange("(u f) -> u f", u=2))
+        nc.gpsimd.memset(eps_col[:], EPS)
+        nc.scalar.activation(out=warm[:], in_=eps_col[:], func=ACT.Sqrt)
+        nc.gpsimd.memset(x_rows[32:64, :], 0.0)
+        nc.gpsimd.memset(x_rows[64:128, :], 0.0)
+        make_identity(nc, ident_bf[:])
+        make_identity(nc, ident_f32[:])
+        nc.gpsimd.dma_start(out=bias_bc[:], in_=b1.partition_broadcast(P))
+        for n0, nw in MX_SLICES:
+            regroup_w(n0, nw)
+
+        x_ps = ps_small.tile([P, P], BF16)
+        nc.tensor.transpose(out=x_ps[:], in_=x_rows[:], identity=ident_bf[:])
+        gb_ps = ps_small.tile([P, P], BF16)
+        nc.tensor.transpose(out=gb_ps[:], in_=gb_rows[:], identity=ident_bf[:])
+
+        for r in range(QUARTERS + 2):
+            if r < QUARTERS:
+                node_plane(r)
+                statistics(r)
+            if r == 1:
+                nc.scalar.copy(out=gb[:], in_=gb_ps[:, 0:4])
+            if r == QUARTERS:
+                for n0, nw in MX_SLICES:
+                    quantise_w(n0, nw)
+            if 1 <= r <= QUARTERS:
+                scale_and_shift(r - 1)
+                normalise(r - 1)
+                transposes(r - 1)
+            if r >= 2:
+                gain_and_bias(r - 2)
+
+        for q in range(QUARTERS + 1):
+            if q < QUARTERS:
+                group(q)
+            if q >= 1:
+                add_bias(2 * q - 2)
+            if q < QUARTERS:
+                quantise(q)
+            if q >= 1:
+                add_bias(2 * q - 1)
+            if q < QUARTERS:
+                multiply(2 * q)
+                multiply(2 * q + 1)
+            if q >= 1:
+                relu_and_store(2 * q - 2)
+                relu_and_store(2 * q - 1)

@@ -75,16 +75,21 @@ def tile_edgeupdaterwrapper_v01_pa_s_kernel(tc, p, x_down, ln_edge_g, ln_edge_b,
         def load_p(q):
             nc.sync.dma_start(out=p_sb[:, tiles_of(q), :], in_=p_rows[:, tiles_of(q), :])
 
-        def statistics(q):
-            for t in range(q * Q_TILES, (q + 1) * Q_TILES):
-                nc.vector.bn_stats(out=stats[:, t, :], in_=p_sb[:, t, :])
-                nc.vector.bn_aggr(out=mean_var[:, t, :], in_=stats[:, t, :])
+        def moments(t):
+            nc.vector.bn_stats(out=stats[:, t, :], in_=p_sb[:, t, :])
+
+        def aggregate(t):
+            nc.vector.bn_aggr(out=mean_var[:, t, :], in_=stats[:, t, :])
+
+        def root(q):
             nc.scalar.activation(
                 out=std[:, tiles_of(q)], in_=mean_var[:, tiles_of(q), 1], func=ACT.Sqrt, bias=eps_col[:], scale=1.0
             )
 
-        def scale_and_shift(q):
+        def invert(q):
             nc.vector.reciprocal(out=rstd[:, tiles_of(q)], in_=std[:, tiles_of(q)])
+
+        def shift_of(q):
             nc.vector.scalar_tensor_tensor(
                 out=shift[:, tiles_of(q)], in0=mean_var[:, tiles_of(q), 0], scalar=-1.0, in1=rstd[:, tiles_of(q)],
                 op0=ALU.mult, op1=ALU.mult,
@@ -142,7 +147,8 @@ def tile_edgeupdaterwrapper_v01_pa_s_kernel(tc, p, x_down, ln_edge_g, ln_edge_b,
 
         def group(q):
             nc.vector.tensor_copy(
-                out=grouped[:, edges_of(q), :], in_=planes[:, :, edges_of(q)].rearrange("q s e -> q e s")
+                out=grouped[:, edges_of(q), :].rearrange("q (c i) s -> q c s i", i=4),
+                in_=planes[:, :, edges_of(q)].rearrange("q s (c i) -> q c s i", i=4),
             )
 
         def quantise(q):
@@ -199,16 +205,28 @@ def tile_edgeupdaterwrapper_v01_pa_s_kernel(tc, p, x_down, ln_edge_g, ln_edge_b,
         nc.tensor.transpose(out=gb_ps[:], in_=gb_rows[:], identity=ident_bf[:])
 
         for r in range(QUARTERS + 2):
-            if r < QUARTERS:
+            taking = r < QUARTERS
+            scaling = 1 <= r <= QUARTERS
+            if taking:
                 node_plane(r)
-                statistics(r)
+                moments(2 * r)
+            if scaling:
+                invert(r - 1)
+            if taking:
+                moments(2 * r + 1)
+                aggregate(2 * r)
+            if r == QUARTERS:
+                quantise_w(*MX_SLICES[0])
+            if scaling:
+                shift_of(r - 1)
+            if taking:
+                aggregate(2 * r + 1)
+                root(r)
+            if r == QUARTERS:
+                quantise_w(*MX_SLICES[1])
             if r == 1:
                 nc.scalar.copy(out=gb[:], in_=gb_ps[:, 0:4])
-            if r == QUARTERS:
-                for n0, nw in MX_SLICES:
-                    quantise_w(n0, nw)
-            if 1 <= r <= QUARTERS:
-                scale_and_shift(r - 1)
+            if scaling:
                 normalise(r - 1)
                 transposes(r - 1)
             if r >= 2:

@@ -48,14 +48,13 @@ def tile_edgeupdaterwrapper_v01_pa_s_kernel(tc, p, x_down, ln_edge_g, ln_edge_b,
         warm = keep.tile([P, 1], F32)
         ident_bf = keep.tile([P, P], BF16)
         ident_f32 = keep.tile([P, P], F32)
+        x_cols = keep.tile([P, NODES], BF16)
         gb = keep.tile([P, 4], F32)
         planes = keep.tile([P, PACK, EDGES], BF16)
         w_grouped = keep.tile([P, F_OUT, PACK], BF16, align_bytes=64)
         w_codes = keep.tile([P, F_OUT], U32, align_bytes=64)
         w_scales = keep.tile([P, F_OUT], U8, align_bytes=64)
-        stats = keep.tile([P, TILES, 6], F32)
-        mean_var = keep.tile([P, TILES, 2], F32)
-        std = keep.tile([P, TILES], F32)
+        stats = keep.tile([P, TILES, 3], F32)
         rstd = keep.tile([P, TILES], F32)
         shift = keep.tile([P, TILES], F32)
         xhat = keep.tile([P, TILES, ED], F32)
@@ -75,23 +74,21 @@ def tile_edgeupdaterwrapper_v01_pa_s_kernel(tc, p, x_down, ln_edge_g, ln_edge_b,
         def load_p(q):
             nc.sync.dma_start(out=p_sb[:, tiles_of(q), :], in_=p_rows[:, tiles_of(q), :])
 
-        def moments(t):
-            nc.vector.bn_stats(out=stats[:, t, :], in_=p_sb[:, t, :])
-
-        def aggregate(t):
-            nc.vector.bn_aggr(out=mean_var[:, t, :], in_=stats[:, t, :])
-
-        def root(q):
-            nc.scalar.activation(
-                out=std[:, tiles_of(q)], in_=mean_var[:, tiles_of(q), 1], func=ACT.Sqrt, bias=eps_col[:], scale=1.0
+        def moments(q):
+            nc.vector.bn_stats(
+                out=stats[:, tiles_of(q), :].rearrange("e t c -> e (t c)"),
+                in_=p_sb[:, tiles_of(q), :].rearrange("e t f -> e f t"),
             )
 
-        def invert(q):
-            nc.vector.reciprocal(out=rstd[:, tiles_of(q)], in_=std[:, tiles_of(q)])
+        def inverse_root(q):
+            nc.scalar.activation(
+                out=rstd[:, tiles_of(q)], in_=stats[:, tiles_of(q), 2], func=ACT.Abs_reciprocal_sqrt,
+                bias=eps_col[:], scale=1.0 / ED,
+            )
 
         def shift_of(q):
             nc.vector.scalar_tensor_tensor(
-                out=shift[:, tiles_of(q)], in0=mean_var[:, tiles_of(q), 0], scalar=-1.0, in1=rstd[:, tiles_of(q)],
+                out=shift[:, tiles_of(q)], in0=stats[:, tiles_of(q), 1], scalar=-1.0, in1=rstd[:, tiles_of(q)],
                 op0=ALU.mult, op1=ALU.mult,
             )
 
@@ -120,6 +117,12 @@ def tile_edgeupdaterwrapper_v01_pa_s_kernel(tc, p, x_down, ln_edge_g, ln_edge_b,
                     scale=gb[:, u : u + 1], bias=gb[:, 2 + u : 3 + u],
                 )
 
+        def gain_and_bias_on_vector(q, u):
+            nc.vector.tensor_scalar(
+                out=planes[:, 2 + u, edges_of(q)], in0=xt_of[q][:, u, :],
+                scalar1=gb[:, u : u + 1], scalar2=gb[:, 2 + u : 3 + u], op0=ALU.mult, op1=ALU.add,
+            )
+
         def regroup_w(n0, nw):
             nc.gpsimd.tensor_scalar(
                 out=w_grouped[:, n0 : n0 + nw, :], in0=w_raw[:, :, n0 : n0 + nw].rearrange("q s n -> q n s"),
@@ -137,16 +140,23 @@ def tile_edgeupdaterwrapper_v01_pa_s_kernel(tc, p, x_down, ln_edge_g, ln_edge_b,
             h, s = divmod(piece, 2)
             es = slice(h * EDGES // 2, (h + 1) * EDGES // 2)
             if s == 0:
-                nodes = x_ps[:, h * NODES // 2 : (h + 1) * NODES // 2].unsqueeze(2)
+                nodes = x_cols[:, h * NODES // 2 : (h + 1) * NODES // 2].unsqueeze(2)
             else:
-                nodes = x_ps[:, 0:NODES].unsqueeze(1)
-            nc.scalar.copy(
+                nodes = x_cols[:, 0:NODES].unsqueeze(1)
+            nc.gpsimd.tensor_scalar(
                 out=planes[:, s, es].rearrange("q (i j) -> q i j", j=NODES),
-                in_=nodes.to_broadcast([P, NODES // 2, NODES]),
+                in0=nodes.to_broadcast([P, NODES // 2, NODES]),
+                scalar1=1.0, scalar2=0.0, op0=ALU.mult, op1=ALU.add,
             )
 
         def group(q):
             nc.vector.tensor_copy(
+                out=grouped[:, edges_of(q), :].rearrange("q (c i) s -> q c s i", i=4),
+                in_=planes[:, :, edges_of(q)].rearrange("q s (c i) -> q c s i", i=4),
+            )
+
+        def group_on_scalar(q):
+            nc.scalar.copy(
                 out=grouped[:, edges_of(q), :].rearrange("q (c i) s -> q c s i", i=4),
                 in_=planes[:, :, edges_of(q)].rearrange("q s (c i) -> q c s i", i=4),
             )
@@ -190,60 +200,83 @@ def tile_edgeupdaterwrapper_v01_pa_s_kernel(tc, p, x_down, ln_edge_g, ln_edge_b,
         nc.scalar.dma_start(out=gb_rows[0:2, :], in_=ln_edge_g.rearrange("(u f) -> u f", u=2))
         nc.scalar.dma_start(out=gb_rows[2:4, :], in_=ln_edge_b.rearrange("(u f) -> u f", u=2))
         nc.gpsimd.memset(eps_col[:], EPS)
-        nc.scalar.activation(out=warm[:], in_=eps_col[:], func=ACT.Sqrt)
+        nc.scalar.activation(out=warm[:], in_=eps_col[:], func=ACT.Abs_reciprocal_sqrt)
         nc.gpsimd.memset(x_rows[32:64, :], 0.0)
         nc.gpsimd.memset(x_rows[64:128, :], 0.0)
         make_identity(nc, ident_bf[:])
         make_identity(nc, ident_f32[:])
         nc.gpsimd.dma_start(out=bias_bc[:], in_=b1.partition_broadcast(P))
-        for n0, nw in MX_SLICES:
-            regroup_w(n0, nw)
 
         x_ps = ps_small.tile([P, P], BF16)
         nc.tensor.transpose(out=x_ps[:], in_=x_rows[:], identity=ident_bf[:])
+        nc.scalar.copy(out=x_cols[:], in_=x_ps[:, 0:NODES])
+        node_plane(0)
+        node_plane(1)
+        for n0, nw in MX_SLICES:
+            regroup_w(n0, nw)
+        node_plane(2)
+        node_plane(3)
         gb_ps = ps_small.tile([P, P], BF16)
         nc.tensor.transpose(out=gb_ps[:], in_=gb_rows[:], identity=ident_bf[:])
 
-        for r in range(QUARTERS + 2):
-            taking = r < QUARTERS
-            scaling = 1 <= r <= QUARTERS
-            if taking:
-                node_plane(r)
-                moments(2 * r)
-            if scaling:
-                invert(r - 1)
-            if taking:
-                moments(2 * r + 1)
-                aggregate(2 * r)
-            if r == QUARTERS:
-                quantise_w(*MX_SLICES[0])
-            if scaling:
-                shift_of(r - 1)
-            if taking:
-                aggregate(2 * r + 1)
-                root(r)
-            if r == QUARTERS:
-                quantise_w(*MX_SLICES[1])
-            if r == 1:
-                nc.scalar.copy(out=gb[:], in_=gb_ps[:, 0:4])
-            if scaling:
-                normalise(r - 1)
-                transposes(r - 1)
-            if r >= 2:
-                gain_and_bias(r - 2)
+        nc.scalar.copy(out=gb[:], in_=gb_ps[:, 0:4])
 
-        for q in range(QUARTERS + 1):
-            if q < QUARTERS:
-                group(q)
-            if q >= 1:
-                add_bias(2 * q - 2)
-            if q < QUARTERS:
-                quantise(q)
-            if q >= 1:
-                add_bias(2 * q - 1)
-            if q < QUARTERS:
-                multiply(2 * q)
-                multiply(2 * q + 1)
-            if q >= 1:
-                relu_and_store(2 * q - 2)
-                relu_and_store(2 * q - 1)
+        def multiply_quarter(q):
+            multiply(2 * q)
+            multiply(2 * q + 1)
+
+        moments(0)
+        inverse_root(0)
+        moments(1)
+        inverse_root(1)
+        shift_of(0)
+        normalise(0)
+        transposes(0)
+        moments(2)
+        inverse_root(2)
+        shift_of(1)
+        normalise(1)
+        transposes(1)
+        moments(3)
+        inverse_root(3)
+        shift_of(2)
+        normalise(2)
+        transposes(2)
+        gain_and_bias_on_vector(0, 0)
+        shift_of(3)
+        gain_and_bias_on_vector(0, 1)
+        gain_and_bias(1)
+        normalise(3)
+        group(0)
+        quantise_w(*MX_SLICES[0])
+        quantise(0)
+        quantise_w(*MX_SLICES[1])
+        multiply_quarter(0)
+        transposes(3)
+        gain_and_bias(2)
+        gain_and_bias(3)
+        group(1)
+        add_bias(0)
+        quantise(1)
+        add_bias(1)
+        multiply_quarter(1)
+        relu_and_store(0)
+        relu_and_store(1)
+        group_on_scalar(3)
+        group(2)
+        add_bias(2)
+        quantise(2)
+        add_bias(3)
+        multiply_quarter(2)
+        relu_and_store(2)
+        relu_and_store(3)
+        quantise(3)
+        multiply_quarter(3)
+        add_bias(4)
+        add_bias(5)
+        relu_and_store(4)
+        relu_and_store(5)
+        add_bias(6)
+        add_bias(7)
+        relu_and_store(6)
+        relu_and_store(7)

@@ -37,7 +37,7 @@ def tile_edgeupdaterwrapper_v01_pa_s_kernel(tc, p, x_down, ln_edge_g, ln_edge_b,
         keep = ctx.enter_context(tc.tile_pool(name="keep", bufs=1))
         ps_small = ctx.enter_context(tc.psum_pool(name="ps_small", bufs=1))
         ps_t = ctx.enter_context(tc.psum_pool(name="ps_t", bufs=3))
-        ps_acc = ctx.enter_context(tc.psum_pool(name="ps_acc", bufs=3))
+        ps_acc = ctx.enter_context(tc.psum_pool(name="ps_acc", bufs=4))
 
         p_sb = keep.tile([P, TILES, ED], BF16)
         x_rows = keep.tile([P, P], BF16)
@@ -48,7 +48,6 @@ def tile_edgeupdaterwrapper_v01_pa_s_kernel(tc, p, x_down, ln_edge_g, ln_edge_b,
         warm = keep.tile([P, 1], F32)
         ident_bf = keep.tile([P, P], BF16)
         ident_f32 = keep.tile([P, P], F32)
-        x_cols = keep.tile([P, NODES], BF16)
         gb = keep.tile([P, 4], F32)
         planes = keep.tile([P, PACK, EDGES], BF16)
         w_grouped = keep.tile([P, F_OUT, PACK], BF16, align_bytes=64)
@@ -117,16 +116,10 @@ def tile_edgeupdaterwrapper_v01_pa_s_kernel(tc, p, x_down, ln_edge_g, ln_edge_b,
                     scale=gb[:, u : u + 1], bias=gb[:, 2 + u : 3 + u],
                 )
 
-        def gain_and_bias_on_vector(q, u):
-            nc.vector.tensor_scalar(
-                out=planes[:, 2 + u, edges_of(q)], in0=xt_of[q][:, u, :],
-                scalar1=gb[:, u : u + 1], scalar2=gb[:, 2 + u : 3 + u], op0=ALU.mult, op1=ALU.add,
-            )
-
         def regroup_w(n0, nw):
-            nc.gpsimd.tensor_scalar(
-                out=w_grouped[:, n0 : n0 + nw, :], in0=w_raw[:, :, n0 : n0 + nw].rearrange("q s n -> q n s"),
-                scalar1=1.0, scalar2=0.0, op0=ALU.mult, op1=ALU.add,
+            nc.vector.tensor_copy(
+                out=w_grouped[:, n0 : n0 + nw, :].rearrange("q (c i) s -> q c s i", i=4),
+                in_=w_raw[:, :, n0 : n0 + nw].rearrange("q s (c i) -> q c s i", i=4),
             )
 
         def quantise_w(n0, nw):
@@ -140,32 +133,28 @@ def tile_edgeupdaterwrapper_v01_pa_s_kernel(tc, p, x_down, ln_edge_g, ln_edge_b,
             h, s = divmod(piece, 2)
             es = slice(h * EDGES // 2, (h + 1) * EDGES // 2)
             if s == 0:
-                nodes = x_cols[:, h * NODES // 2 : (h + 1) * NODES // 2].unsqueeze(2)
+                nodes = small_ps[:, 0, h * NODES // 2 : (h + 1) * NODES // 2].unsqueeze(2)
             else:
-                nodes = x_cols[:, 0:NODES].unsqueeze(1)
-            nc.gpsimd.tensor_scalar(
-                out=planes[:, s, es].rearrange("q (i j) -> q i j", j=NODES),
-                in0=nodes.to_broadcast([P, NODES // 2, NODES]),
-                scalar1=1.0, scalar2=0.0, op0=ALU.mult, op1=ALU.add,
-            )
-
-        def group(q):
-            nc.vector.tensor_copy(
-                out=grouped[:, edges_of(q), :].rearrange("q (c i) s -> q c s i", i=4),
-                in_=planes[:, :, edges_of(q)].rearrange("q s (c i) -> q c s i", i=4),
-            )
-
-        def group_on_scalar(q):
+                nodes = small_ps[:, 0, 0:NODES].unsqueeze(1)
             nc.scalar.copy(
-                out=grouped[:, edges_of(q), :].rearrange("q (c i) s -> q c s i", i=4),
-                in_=planes[:, :, edges_of(q)].rearrange("q s (c i) -> q c s i", i=4),
+                out=planes[:, s, es].rearrange("q (i j) -> q i j", j=NODES),
+                in_=nodes.to_broadcast([P, NODES // 2, NODES]),
             )
 
-        def quantise(q):
+        def tile_edges(t):
+            return slice(t * P, (t + 1) * P)
+
+        def group(t):
+            nc.vector.tensor_copy(
+                out=grouped[:, tile_edges(t), :].rearrange("q (c i) s -> q c s i", i=4),
+                in_=planes[:, :, tile_edges(t)].rearrange("q s (c i) -> q c s i", i=4),
+            )
+
+        def quantise(t):
             nc.vector.quantize_mx(
-                out=z_codes[:, edges_of(q)].bitcast(FP8X4),
-                scales=z_scales[:, edges_of(q)],
-                in_=grouped[:, edges_of(q), :].rearrange("q e s -> q (e s)"),
+                out=z_codes[:, tile_edges(t)].bitcast(FP8X4),
+                scales=z_scales[:, tile_edges(t)],
+                in_=grouped[:, tile_edges(t), :].rearrange("q e s -> q (e s)"),
             )
 
         def multiply(t):
@@ -207,26 +196,14 @@ def tile_edgeupdaterwrapper_v01_pa_s_kernel(tc, p, x_down, ln_edge_g, ln_edge_b,
         make_identity(nc, ident_f32[:])
         nc.gpsimd.dma_start(out=bias_bc[:], in_=b1.partition_broadcast(P))
 
-        x_ps = ps_small.tile([P, P], BF16)
-        nc.tensor.transpose(out=x_ps[:], in_=x_rows[:], identity=ident_bf[:])
-        nc.scalar.copy(out=x_cols[:], in_=x_ps[:, 0:NODES])
+        small_ps = ps_small.tile([P, 2, P], BF16)
+        nc.tensor.transpose(out=small_ps[:, 0, :], in_=x_rows[:], identity=ident_bf[:])
+        nc.tensor.transpose(out=small_ps[:, 1, :], in_=gb_rows[:], identity=ident_bf[:])
+
         node_plane(0)
-        node_plane(1)
-        for n0, nw in MX_SLICES:
-            regroup_w(n0, nw)
-        node_plane(2)
-        node_plane(3)
-        gb_ps = ps_small.tile([P, P], BF16)
-        nc.tensor.transpose(out=gb_ps[:], in_=gb_rows[:], identity=ident_bf[:])
-
-        nc.scalar.copy(out=gb[:], in_=gb_ps[:, 0:4])
-
-        def multiply_quarter(q):
-            multiply(2 * q)
-            multiply(2 * q + 1)
-
         moments(0)
         inverse_root(0)
+        node_plane(1)
         moments(1)
         inverse_root(1)
         shift_of(0)
@@ -242,41 +219,32 @@ def tile_edgeupdaterwrapper_v01_pa_s_kernel(tc, p, x_down, ln_edge_g, ln_edge_b,
         shift_of(2)
         normalise(2)
         transposes(2)
-        gain_and_bias_on_vector(0, 0)
+        regroup_w(*MX_SLICES[0])
         shift_of(3)
-        gain_and_bias_on_vector(0, 1)
+        regroup_w(*MX_SLICES[1])
+        quantise_w(*MX_SLICES[0])
+        quantise_w(*MX_SLICES[1])
+        nc.scalar.copy(out=gb[:], in_=small_ps[:, 1, 0:4])
+        gain_and_bias(0)
         gain_and_bias(1)
         normalise(3)
-        group(0)
-        quantise_w(*MX_SLICES[0])
-        quantise(0)
-        quantise_w(*MX_SLICES[1])
-        multiply_quarter(0)
-        transposes(3)
-        gain_and_bias(2)
-        gain_and_bias(3)
-        group(1)
-        add_bias(0)
-        quantise(1)
-        add_bias(1)
-        multiply_quarter(1)
-        relu_and_store(0)
-        relu_and_store(1)
-        group_on_scalar(3)
-        group(2)
-        add_bias(2)
-        quantise(2)
-        add_bias(3)
-        multiply_quarter(2)
-        relu_and_store(2)
-        relu_and_store(3)
-        quantise(3)
-        multiply_quarter(3)
-        add_bias(4)
-        add_bias(5)
-        relu_and_store(4)
-        relu_and_store(5)
-        add_bias(6)
-        add_bias(7)
-        relu_and_store(6)
-        relu_and_store(7)
+        node_plane(2)
+        node_plane(3)
+        for q in range(QUARTERS + 1):
+            if q < QUARTERS:
+                group(2 * q)
+                group(2 * q + 1)
+                quantise(2 * q)
+                quantise(2 * q + 1)
+                multiply(2 * q)
+                multiply(2 * q + 1)
+            if q == 0:
+                transposes(3)
+                gain_and_bias(2)
+            if q >= 1:
+                add_bias(2 * q - 2)
+                add_bias(2 * q - 1)
+                relu_and_store(2 * q - 2)
+                relu_and_store(2 * q - 1)
+            if q == 1:
+                gain_and_bias(3)

@@ -91,28 +91,41 @@ def tile_edgeupdaterwrapper_v01_pa_s_kernel(tc, p, x_down, ln_edge_g, ln_edge_b,
                 op0=ALU.mult, op1=ALU.mult,
             )
 
+        def normalise_tile(t):
+            nc.scalar.activation(
+                out=xhat[:, t, :], in_=p_sb[:, t, :], func=ACT.Identity,
+                scale=rstd[:, t : t + 1], bias=shift[:, t : t + 1],
+            )
+
         def normalise(q):
-            for t in range(q * Q_TILES, (q + 1) * Q_TILES):
-                nc.scalar.activation(
-                    out=xhat[:, t, :], in_=p_sb[:, t, :], func=ACT.Identity,
-                    scale=rstd[:, t : t + 1], bias=shift[:, t : t + 1],
+            normalise_tile(2 * q)
+            normalise_tile(2 * q + 1)
+
+        def transpose_tile(t):
+            q, c = divmod(t, Q_TILES)
+            if c == 0:
+                xt_of[q] = ps_t.tile([P, 2, Q_EDGES], F32, name="xt")
+            for u in range(2):
+                nc.tensor.transpose(
+                    out=xt_of[q][:, u, c * P : (c + 1) * P], in_=xhat[:, t, u * P : (u + 1) * P], identity=ident_f32[:]
                 )
 
         def transposes(q):
-            xt = ps_t.tile([P, 2, Q_EDGES], F32, name="xt")
-            xt_of[q] = xt
-            for u in range(2):
-                for c in range(Q_TILES):
-                    nc.tensor.transpose(
-                        out=xt[:, u, c * P : (c + 1) * P],
-                        in_=xhat[:, q * Q_TILES + c, u * P : (u + 1) * P],
-                        identity=ident_f32[:],
-                    )
+            transpose_tile(2 * q)
+            transpose_tile(2 * q + 1)
 
         def gain_and_bias(q):
             for u in range(2):
                 nc.scalar.activation(
                     out=planes[:, 2 + u, edges_of(q)], in_=xt_of[q][:, u, :], func=ACT.Identity,
+                    scale=gb[:, u : u + 1], bias=gb[:, 2 + u : 3 + u],
+                )
+
+        def gain_and_bias_tile(t):
+            q, c = divmod(t, Q_TILES)
+            for u in range(2):
+                nc.scalar.activation(
+                    out=planes[:, 2 + u, tile_edges(t)], in_=xt_of[q][:, u, c * P : (c + 1) * P], func=ACT.Identity,
                     scale=gb[:, u : u + 1], bias=gb[:, 2 + u : 3 + u],
                 )
 
@@ -129,17 +142,13 @@ def tile_edgeupdaterwrapper_v01_pa_s_kernel(tc, p, x_down, ln_edge_g, ln_edge_b,
                 in_=w_grouped[:, n0 : n0 + nw, :].rearrange("q n s -> q (n s)"),
             )
 
-        def node_plane(piece):
-            h, s = divmod(piece, 2)
-            es = slice(h * EDGES // 2, (h + 1) * EDGES // 2)
-            if s == 0:
-                nodes = small_ps[:, 0, h * NODES // 2 : (h + 1) * NODES // 2].unsqueeze(2)
-            else:
-                nodes = small_ps[:, 0, 0:NODES].unsqueeze(1)
-            nc.scalar.copy(
-                out=planes[:, s, es].rearrange("q (i j) -> q i j", j=NODES),
-                in_=nodes.to_broadcast([P, NODES // 2, NODES]),
-            )
+        def node_planes(i0, i1):
+            es = slice(i0 * NODES, i1 * NODES)
+            for s, nodes in ((0, small_ps[:, 0, i0:i1].unsqueeze(2)), (1, small_ps[:, 0, 0:NODES].unsqueeze(1))):
+                nc.scalar.copy(
+                    out=planes[:, s, es].rearrange("q (i j) -> q i j", j=NODES),
+                    in_=nodes.to_broadcast([P, i1 - i0, NODES]),
+                )
 
         def tile_edges(t):
             return slice(t * P, (t + 1) * P)
@@ -179,12 +188,10 @@ def tile_edgeupdaterwrapper_v01_pa_s_kernel(tc, p, x_down, ln_edge_g, ln_edge_b,
             nc.scalar.activation(out=result[:, t, :], in_=result[:, t, :], func=ACT.Relu)
             nc.sync.dma_start(out=out_rows[:, t, :], in_=result[:, t, :])
 
-        nc.sync.dma_start(out=x_rows[0:NODES, :], in_=x_down.flatten_outer_dims())
-        load_p(0)
-        load_p(1)
+        for q in range(QUARTERS):
+            load_p(q)
         nc.sync.dma_start(out=w_raw[:], in_=W1.rearrange("(s q) n -> q s n", q=P))
-        load_p(2)
-        load_p(3)
+        nc.scalar.dma_start(out=x_rows[0:NODES, :], in_=x_down.flatten_outer_dims())
         nc.gpsimd.memset(gb_rows[:], 0.0)
         nc.scalar.dma_start(out=gb_rows[0:2, :], in_=ln_edge_g.rearrange("(u f) -> u f", u=2))
         nc.scalar.dma_start(out=gb_rows[2:4, :], in_=ln_edge_b.rearrange("(u f) -> u f", u=2))
@@ -200,23 +207,27 @@ def tile_edgeupdaterwrapper_v01_pa_s_kernel(tc, p, x_down, ln_edge_g, ln_edge_b,
         nc.tensor.transpose(out=small_ps[:, 0, :], in_=x_rows[:], identity=ident_bf[:])
         nc.tensor.transpose(out=small_ps[:, 1, :], in_=gb_rows[:], identity=ident_bf[:])
 
-        node_plane(0)
         moments(0)
         inverse_root(0)
-        node_plane(1)
+        nc.scalar.copy(out=gb[:], in_=small_ps[:, 1, 0:4])
         moments(1)
         inverse_root(1)
         shift_of(0)
-        normalise(0)
-        transposes(0)
+        normalise_tile(0)
+        transpose_tile(0)
+        normalise_tile(1)
+        transpose_tile(1)
         moments(2)
         inverse_root(2)
         shift_of(1)
         normalise(1)
         transposes(1)
+        node_planes(0, Q_NODES)
         moments(3)
         inverse_root(3)
         shift_of(2)
+        gain_and_bias_tile(0)
+        gain_and_bias_tile(1)
         normalise(2)
         transposes(2)
         regroup_w(*MX_SLICES[0])
@@ -224,12 +235,10 @@ def tile_edgeupdaterwrapper_v01_pa_s_kernel(tc, p, x_down, ln_edge_g, ln_edge_b,
         regroup_w(*MX_SLICES[1])
         quantise_w(*MX_SLICES[0])
         quantise_w(*MX_SLICES[1])
-        nc.scalar.copy(out=gb[:], in_=small_ps[:, 1, 0:4])
-        gain_and_bias(0)
+        node_planes(Q_NODES, 2 * Q_NODES)
         gain_and_bias(1)
         normalise(3)
-        node_plane(2)
-        node_plane(3)
+        node_planes(2 * Q_NODES, NODES)
         for q in range(QUARTERS + 1):
             if q < QUARTERS:
                 group(2 * q)

@@ -166,6 +166,19 @@ def tile_edgeupdaterwrapper_v01_pa_s_kernel(tc, p, x_down, ln_edge_g, ln_edge_b,
                 in_=grouped[:, tile_edges(t), :].rearrange("q e s -> q (e s)"),
             )
 
+        def group_quarter(q):
+            nc.vector.tensor_copy(
+                out=grouped[:, edges_of(q), :].rearrange("q (c i) s -> q c s i", i=4),
+                in_=planes[:, :, edges_of(q)].rearrange("q s (c i) -> q c s i", i=4),
+            )
+
+        def quantise_quarter(q):
+            nc.vector.quantize_mx(
+                out=z_codes[:, edges_of(q)].bitcast(FP8X4),
+                scales=z_scales[:, edges_of(q)],
+                in_=grouped[:, edges_of(q), :].rearrange("q e s -> q (e s)"),
+            )
+
         def multiply(t):
             acc = ps_acc.tile([P, 512], F32, name="acc")
             acc_of[t] = acc
@@ -239,21 +252,33 @@ def tile_edgeupdaterwrapper_v01_pa_s_kernel(tc, p, x_down, ln_edge_g, ln_edge_b,
         gain_and_bias(1)
         normalise(3)
         node_planes(2 * Q_NODES, NODES)
-        for q in range(QUARTERS + 1):
-            if q < QUARTERS:
-                group(2 * q)
-                group(2 * q + 1)
-                quantise(2 * q)
-                quantise(2 * q + 1)
-                multiply(2 * q)
-                multiply(2 * q + 1)
+        for q in range(2):
+            group(2 * q)
+            group(2 * q + 1)
+            quantise(2 * q)
+            quantise(2 * q + 1)
+            multiply(2 * q)
+            multiply(2 * q + 1)
             if q == 0:
                 transposes(3)
                 gain_and_bias(2)
-            if q >= 1:
-                add_bias(2 * q - 2)
-                add_bias(2 * q - 1)
-                relu_and_store(2 * q - 2)
-                relu_and_store(2 * q - 1)
-            if q == 1:
                 gain_and_bias(3)
+        add_bias(0)
+        add_bias(1)
+        relu_and_store(0)
+        relu_and_store(1)
+        group_quarter(2)
+        add_bias(2)
+        quantise_quarter(2)
+        multiply(4)
+        multiply(5)
+        group_quarter(3)
+        add_bias(3)
+        quantise_quarter(3)
+        multiply(6)
+        multiply(7)
+        relu_and_store(2)
+        relu_and_store(3)
+        for t in range(4, TILES):
+            add_bias(t)
+            relu_and_store(t)

@@ -49,7 +49,7 @@ def tile_edgeupdaterwrapper_v01_pa_s_kernel(tc, p, x_down, ln_edge_g, ln_edge_b,
         ident_bf = keep.tile([P, P], BF16)
         ident_f32 = keep.tile([P, P], F32)
         gb = keep.tile([P, 4], F32)
-        planes = keep.tile([P, PACK, EDGES], BF16)
+        planes = keep.tile([P, 2, PACK, Q_EDGES], BF16)
         w_grouped = keep.tile([P, F_OUT, PACK], BF16, align_bytes=64)
         w_codes = keep.tile([P, F_OUT], U32, align_bytes=64)
         w_scales = keep.tile([P, F_OUT], U8, align_bytes=64)
@@ -117,7 +117,7 @@ def tile_edgeupdaterwrapper_v01_pa_s_kernel(tc, p, x_down, ln_edge_g, ln_edge_b,
         def gain_and_bias(q):
             for u in range(2):
                 nc.scalar.activation(
-                    out=planes[:, 2 + u, edges_of(q)], in_=xt_of[q][:, u, :], func=ACT.Identity,
+                    out=planes[:, q % 2, 2 + u, :], in_=xt_of[q][:, u, :], func=ACT.Identity,
                     scale=gb[:, u : u + 1], bias=gb[:, 2 + u : 3 + u],
                 )
 
@@ -125,7 +125,7 @@ def tile_edgeupdaterwrapper_v01_pa_s_kernel(tc, p, x_down, ln_edge_g, ln_edge_b,
             q, c = divmod(t, Q_TILES)
             for u in range(2):
                 nc.scalar.activation(
-                    out=planes[:, 2 + u, tile_edges(t)], in_=xt_of[q][:, u, c * P : (c + 1) * P], func=ACT.Identity,
+                    out=planes[:, q % 2, 2 + u, c * P : (c + 1) * P], in_=xt_of[q][:, u, c * P : (c + 1) * P], func=ACT.Identity,
                     scale=gb[:, u : u + 1], bias=gb[:, 2 + u : 3 + u],
                 )
 
@@ -142,13 +142,16 @@ def tile_edgeupdaterwrapper_v01_pa_s_kernel(tc, p, x_down, ln_edge_g, ln_edge_b,
                 in_=w_grouped[:, n0 : n0 + nw, :].rearrange("q n s -> q (n s)"),
             )
 
-        def node_planes(i0, i1):
-            es = slice(i0 * NODES, i1 * NODES)
-            for s, nodes in ((0, small_ps[:, 0, i0:i1].unsqueeze(2)), (1, small_ps[:, 0, 0:NODES].unsqueeze(1))):
-                nc.scalar.copy(
-                    out=planes[:, s, es].rearrange("q (i j) -> q i j", j=NODES),
-                    in_=nodes.to_broadcast([P, i1 - i0, NODES]),
-                )
+        def node_plane(h, s, nodes):
+            nc.scalar.copy(
+                out=planes[:, h, s, :].rearrange("q (i j) -> q i j", j=NODES), in_=nodes.to_broadcast([P, Q_NODES, NODES])
+            )
+
+        def x_i_plane(q):
+            node_plane(q % 2, 0, small_ps[:, 0, q * Q_NODES : (q + 1) * Q_NODES].unsqueeze(2))
+
+        def x_j_plane(h):
+            node_plane(h, 1, small_ps[:, 0, 0:NODES].unsqueeze(1))
 
         def tile_edges(t):
             return slice(t * P, (t + 1) * P)
@@ -156,7 +159,7 @@ def tile_edgeupdaterwrapper_v01_pa_s_kernel(tc, p, x_down, ln_edge_g, ln_edge_b,
         def group(t):
             nc.vector.tensor_copy(
                 out=grouped[:, tile_edges(t), :].rearrange("q (c i) s -> q c s i", i=4),
-                in_=planes[:, :, tile_edges(t)].rearrange("q s (c i) -> q c s i", i=4),
+                in_=planes[:, (t // 2) % 2, :, (t % 2) * P : (t % 2 + 1) * P].rearrange("q s (c i) -> q c s i", i=4),
             )
 
         def quantise(t):
@@ -169,7 +172,7 @@ def tile_edgeupdaterwrapper_v01_pa_s_kernel(tc, p, x_down, ln_edge_g, ln_edge_b,
         def group_quarter(q):
             nc.vector.tensor_copy(
                 out=grouped[:, edges_of(q), :].rearrange("q (c i) s -> q c s i", i=4),
-                in_=planes[:, :, edges_of(q)].rearrange("q s (c i) -> q c s i", i=4),
+                in_=planes[:, q % 2, :, :].rearrange("q s (c i) -> q c s i", i=4),
             )
 
         def quantise_quarter(q):
@@ -235,7 +238,8 @@ def tile_edgeupdaterwrapper_v01_pa_s_kernel(tc, p, x_down, ln_edge_g, ln_edge_b,
         shift_of(1)
         normalise(1)
         transposes(1)
-        node_planes(0, Q_NODES)
+        x_i_plane(0)
+        x_j_plane(0)
         moments(3)
         inverse_root(3)
         shift_of(2)
@@ -248,10 +252,10 @@ def tile_edgeupdaterwrapper_v01_pa_s_kernel(tc, p, x_down, ln_edge_g, ln_edge_b,
         regroup_w(*MX_SLICES[1])
         quantise_w(*MX_SLICES[0])
         quantise_w(*MX_SLICES[1])
-        node_planes(Q_NODES, 2 * Q_NODES)
+        x_i_plane(1)
+        x_j_plane(1)
         gain_and_bias(1)
         normalise(3)
-        node_planes(2 * Q_NODES, NODES)
         for q in range(2):
             group(2 * q)
             group(2 * q + 1)
@@ -259,10 +263,10 @@ def tile_edgeupdaterwrapper_v01_pa_s_kernel(tc, p, x_down, ln_edge_g, ln_edge_b,
             quantise(2 * q + 1)
             multiply(2 * q)
             multiply(2 * q + 1)
+            x_i_plane(q + 2)
             if q == 0:
                 transposes(3)
-                gain_and_bias(2)
-                gain_and_bias(3)
+            gain_and_bias(q + 2)
         add_bias(0)
         add_bias(1)
         relu_and_store(0)
@@ -279,6 +283,13 @@ def tile_edgeupdaterwrapper_v01_pa_s_kernel(tc, p, x_down, ln_edge_g, ln_edge_b,
         multiply(7)
         relu_and_store(2)
         relu_and_store(3)
+        def relu_on_vector_and_store(t):
+            nc.vector.tensor_scalar(out=result[:, t, :], in0=result[:, t, :], scalar1=0.0, scalar2=None, op0=ALU.max)
+            nc.sync.dma_start(out=out_rows[:, t, :], in_=result[:, t, :])
+
         for t in range(4, TILES):
             add_bias(t)
-            relu_and_store(t)
+        relu_and_store(4)
+        relu_and_store(5)
+        relu_on_vector_and_store(6)
+        relu_on_vector_and_store(7)

@@ -49,7 +49,7 @@ def tile_edgeupdaterwrapper_v01_pa_s_kernel(tc, p, x_down, ln_edge_g, ln_edge_b,
         ident_bf = keep.tile([P, P], BF16)
         ident_f32 = keep.tile([P, P], F32)
         gb = keep.tile([P, 4], F32)
-        planes = keep.tile([P, 2, PACK, Q_EDGES], BF16)
+        planes = keep.tile([P, 10, Q_EDGES], BF16)
         w_grouped = keep.tile([P, F_OUT, PACK], BF16, align_bytes=64)
         w_codes = keep.tile([P, F_OUT], U32, align_bytes=64)
         w_scales = keep.tile([P, F_OUT], U8, align_bytes=64)
@@ -63,6 +63,12 @@ def tile_edgeupdaterwrapper_v01_pa_s_kernel(tc, p, x_down, ln_edge_g, ln_edge_b,
         result = keep.tile([P, TILES, F_OUT], F32)
         xt_of = {}
         acc_of = {}
+
+        def places_of(q):
+            return slice(2, 6) if q % 2 == 0 else slice(0, 10, 3)
+
+        def place_of(q, s):
+            return 2 + s if q % 2 == 0 else 3 * s
 
         def tiles_of(q):
             return slice(q * Q_TILES, (q + 1) * Q_TILES)
@@ -117,7 +123,7 @@ def tile_edgeupdaterwrapper_v01_pa_s_kernel(tc, p, x_down, ln_edge_g, ln_edge_b,
         def gain_and_bias(q):
             for u in range(2):
                 nc.scalar.activation(
-                    out=planes[:, q % 2, 2 + u, :], in_=xt_of[q][:, u, :], func=ACT.Identity,
+                    out=planes[:, place_of(q, 2 + u), :], in_=xt_of[q][:, u, :], func=ACT.Identity,
                     scale=gb[:, u : u + 1], bias=gb[:, 2 + u : 3 + u],
                 )
 
@@ -125,7 +131,7 @@ def tile_edgeupdaterwrapper_v01_pa_s_kernel(tc, p, x_down, ln_edge_g, ln_edge_b,
             q, c = divmod(t, Q_TILES)
             for u in range(2):
                 nc.scalar.activation(
-                    out=planes[:, q % 2, 2 + u, c * P : (c + 1) * P], in_=xt_of[q][:, u, c * P : (c + 1) * P], func=ACT.Identity,
+                    out=planes[:, place_of(q, 2 + u), c * P : (c + 1) * P], in_=xt_of[q][:, u, c * P : (c + 1) * P], func=ACT.Identity,
                     scale=gb[:, u : u + 1], bias=gb[:, 2 + u : 3 + u],
                 )
 
@@ -142,16 +148,16 @@ def tile_edgeupdaterwrapper_v01_pa_s_kernel(tc, p, x_down, ln_edge_g, ln_edge_b,
                 in_=w_grouped[:, n0 : n0 + nw, :].rearrange("q n s -> q (n s)"),
             )
 
-        def node_plane(h, s, nodes):
+        def node_plane(place, nodes):
             nc.scalar.copy(
-                out=planes[:, h, s, :].rearrange("q (i j) -> q i j", j=NODES), in_=nodes.to_broadcast([P, Q_NODES, NODES])
+                out=planes[:, place, :].rearrange("q (i j) -> q i j", j=NODES), in_=nodes.to_broadcast([P, Q_NODES, NODES])
             )
 
         def x_i_plane(q):
-            node_plane(q % 2, 0, small_ps[:, 0, q * Q_NODES : (q + 1) * Q_NODES].unsqueeze(2))
+            node_plane(place_of(q, 0), small_ps[:, 0, q * Q_NODES : (q + 1) * Q_NODES].unsqueeze(2))
 
-        def x_j_plane(h):
-            node_plane(h, 1, small_ps[:, 0, 0:NODES].unsqueeze(1))
+        def x_j_plane():
+            node_plane(place_of(0, 1), small_ps[:, 0, 0:NODES].unsqueeze(1))
 
         def tile_edges(t):
             return slice(t * P, (t + 1) * P)
@@ -159,7 +165,7 @@ def tile_edgeupdaterwrapper_v01_pa_s_kernel(tc, p, x_down, ln_edge_g, ln_edge_b,
         def group(t):
             nc.vector.tensor_copy(
                 out=grouped[:, tile_edges(t), :].rearrange("q (c i) s -> q c s i", i=4),
-                in_=planes[:, (t // 2) % 2, :, (t % 2) * P : (t % 2 + 1) * P].rearrange("q s (c i) -> q c s i", i=4),
+                in_=planes[:, places_of(t // 2), (t % 2) * P : (t % 2 + 1) * P].rearrange("q s (c i) -> q c s i", i=4),
             )
 
         def quantise(t):
@@ -172,7 +178,7 @@ def tile_edgeupdaterwrapper_v01_pa_s_kernel(tc, p, x_down, ln_edge_g, ln_edge_b,
         def group_quarter(q):
             nc.vector.tensor_copy(
                 out=grouped[:, edges_of(q), :].rearrange("q (c i) s -> q c s i", i=4),
-                in_=planes[:, q % 2, :, :].rearrange("q s (c i) -> q c s i", i=4),
+                in_=planes[:, places_of(q), :].rearrange("q s (c i) -> q c s i", i=4),
             )
 
         def quantise_quarter(q):
@@ -239,7 +245,7 @@ def tile_edgeupdaterwrapper_v01_pa_s_kernel(tc, p, x_down, ln_edge_g, ln_edge_b,
         normalise(1)
         transposes(1)
         x_i_plane(0)
-        x_j_plane(0)
+        x_j_plane()
         moments(3)
         inverse_root(3)
         shift_of(2)
@@ -253,7 +259,6 @@ def tile_edgeupdaterwrapper_v01_pa_s_kernel(tc, p, x_down, ln_edge_g, ln_edge_b,
         quantise_w(*MX_SLICES[0])
         quantise_w(*MX_SLICES[1])
         x_i_plane(1)
-        x_j_plane(1)
         gain_and_bias(1)
         normalise(3)
         for q in range(2):

@@ -232,6 +232,7 @@ def tile_edgeupdaterwrapper_v01_pa_s_kernel(tc, p, x_down, ln_edge_g, ln_edge_b,
         moments(0)
         inverse_root(0)
         nc.scalar.copy(out=gb[:], in_=small_ps[:, 1, 0:4])
+        x_j_plane()
         moments(1)
         inverse_root(1)
         shift_of(0)
@@ -245,7 +246,7 @@ def tile_edgeupdaterwrapper_v01_pa_s_kernel(tc, p, x_down, ln_edge_g, ln_edge_b,
         normalise(1)
         transposes(1)
         x_i_plane(0)
-        x_j_plane()
+        x_i_plane(1)
         moments(3)
         inverse_root(3)
         shift_of(2)
@@ -258,7 +259,6 @@ def tile_edgeupdaterwrapper_v01_pa_s_kernel(tc, p, x_down, ln_edge_g, ln_edge_b,
         regroup_w(*MX_SLICES[1])
         quantise_w(*MX_SLICES[0])
         quantise_w(*MX_SLICES[1])
-        x_i_plane(1)
         gain_and_bias(1)
         normalise(3)
         for q in range(2):

@@ -23,6 +23,8 @@ Q_TILES = TILES // QUARTERS
 Q_EDGES = Q_TILES * P
 Q_NODES = NODES // QUARTERS
 EPS = 1e-5
+X_J = 5
+STEPS = (1, 3, 4, 5)
 MX_SLICES = ((0, 256), (256, 128))
 FLOPS = 2 * EDGES * PACK * P * F_OUT
 
@@ -49,7 +51,7 @@ def tile_edgeupdaterwrapper_v01_pa_s_kernel(tc, p, x_down, ln_edge_g, ln_edge_b,
         ident_bf = keep.tile([P, P], BF16)
         ident_f32 = keep.tile([P, P], F32)
         gb = keep.tile([P, 4], F32)
-        planes = keep.tile([P, 10, Q_EDGES], BF16)
+        planes = keep.tile([P, X_J + 2 * STEPS[-1] + 1, Q_EDGES], BF16)
         w_grouped = keep.tile([P, F_OUT, PACK], BF16, align_bytes=64)
         w_codes = keep.tile([P, F_OUT], U32, align_bytes=64)
         w_scales = keep.tile([P, F_OUT], U8, align_bytes=64)
@@ -65,10 +67,10 @@ def tile_edgeupdaterwrapper_v01_pa_s_kernel(tc, p, x_down, ln_edge_g, ln_edge_b,
         acc_of = {}
 
         def places_of(q):
-            return slice(2, 6) if q % 2 == 0 else slice(0, 10, 3)
+            return slice(X_J - STEPS[q], X_J + 2 * STEPS[q] + 1, STEPS[q])
 
         def place_of(q, s):
-            return 2 + s if q % 2 == 0 else 3 * s
+            return X_J + (s - 1) * STEPS[q]
 
         def tiles_of(q):
             return slice(q * Q_TILES, (q + 1) * Q_TILES)
@@ -103,9 +105,16 @@ def tile_edgeupdaterwrapper_v01_pa_s_kernel(tc, p, x_down, ln_edge_g, ln_edge_b,
                 scale=rstd[:, t : t + 1], bias=shift[:, t : t + 1],
             )
 
-        def normalise(q):
-            normalise_tile(2 * q)
-            normalise_tile(2 * q + 1)
+        def normalise_on_scalar(q):
+            for t in (2 * q, 2 * q + 1):
+                normalise_tile(t)
+
+        def normalise_on_vector(q):
+            for t in (2 * q, 2 * q + 1):
+                nc.vector.tensor_scalar(
+                    out=xhat[:, t, :], in0=p_sb[:, t, :], scalar1=stats[:, t, 1:2], scalar2=rstd[:, t : t + 1],
+                    op0=ALU.subtract, op1=ALU.mult,
+                )
 
         def transpose_tile(t):
             q, c = divmod(t, Q_TILES)
@@ -141,6 +150,12 @@ def tile_edgeupdaterwrapper_v01_pa_s_kernel(tc, p, x_down, ln_edge_g, ln_edge_b,
                 in_=w_raw[:, :, n0 : n0 + nw].rearrange("q s (c i) -> q c s i", i=4),
             )
 
+        def regroup_w_scalar(n0, nw):
+            nc.scalar.copy(
+                out=w_grouped[:, n0 : n0 + nw, :].rearrange("q (c i) s -> q c s i", i=4),
+                in_=w_raw[:, :, n0 : n0 + nw].rearrange("q s (c i) -> q c s i", i=4),
+            )
+
         def quantise_w(n0, nw):
             nc.vector.quantize_mx(
                 out=w_codes[:, n0 : n0 + nw].bitcast(FP8X4),
@@ -168,24 +183,17 @@ def tile_edgeupdaterwrapper_v01_pa_s_kernel(tc, p, x_down, ln_edge_g, ln_edge_b,
                 in_=planes[:, places_of(t // 2), (t % 2) * P : (t % 2 + 1) * P].rearrange("q s (c i) -> q c s i", i=4),
             )
 
+        def group_scalar(t):
+            nc.scalar.copy(
+                out=grouped[:, tile_edges(t), :].rearrange("q (c i) s -> q c s i", i=4),
+                in_=planes[:, places_of(t // 2), (t % 2) * P : (t % 2 + 1) * P].rearrange("q s (c i) -> q c s i", i=4),
+            )
+
         def quantise(t):
             nc.vector.quantize_mx(
                 out=z_codes[:, tile_edges(t)].bitcast(FP8X4),
                 scales=z_scales[:, tile_edges(t)],
                 in_=grouped[:, tile_edges(t), :].rearrange("q e s -> q (e s)"),
-            )
-
-        def group_quarter(q):
-            nc.vector.tensor_copy(
-                out=grouped[:, edges_of(q), :].rearrange("q (c i) s -> q c s i", i=4),
-                in_=planes[:, places_of(q), :].rearrange("q s (c i) -> q c s i", i=4),
-            )
-
-        def quantise_quarter(q):
-            nc.vector.quantize_mx(
-                out=z_codes[:, edges_of(q)].bitcast(FP8X4),
-                scales=z_scales[:, edges_of(q)],
-                in_=grouped[:, edges_of(q), :].rearrange("q e s -> q (e s)"),
             )
 
         def multiply(t):
@@ -210,8 +218,19 @@ def tile_edgeupdaterwrapper_v01_pa_s_kernel(tc, p, x_down, ln_edge_g, ln_edge_b,
             nc.scalar.activation(out=result[:, t, :], in_=result[:, t, :], func=ACT.Relu)
             nc.sync.dma_start(out=out_rows[:, t, :], in_=result[:, t, :])
 
-        for q in range(QUARTERS):
-            load_p(q)
+        def store(t):
+            nc.sync.dma_start(out=out_rows[:, t, :], in_=result[:, t, :])
+
+        def add_bias_columns(t, n0, n1):
+            nc.vector.tensor_tensor(out=result[:, t, n0:n1], in0=acc_of[t][:, n0:n1], in1=bias_bc[:, n0:n1], op=ALU.add)
+
+        def relu_columns_on_vector(t, n0, n1):
+            nc.vector.tensor_scalar(out=result[:, t, n0:n1], in0=result[:, t, n0:n1], scalar1=0.0, scalar2=None, op0=ALU.max)
+
+        load_p(0)
+        load_p(1)
+        load_p(2)
+        load_p(3)
         nc.sync.dma_start(out=w_raw[:], in_=W1.rearrange("(s q) n -> q s n", q=P))
         nc.scalar.dma_start(out=x_rows[0:NODES, :], in_=x_down.flatten_outer_dims())
         nc.gpsimd.memset(gb_rows[:], 0.0)
@@ -228,7 +247,6 @@ def tile_edgeupdaterwrapper_v01_pa_s_kernel(tc, p, x_down, ln_edge_g, ln_edge_b,
         small_ps = ps_small.tile([P, 2, P], BF16)
         nc.tensor.transpose(out=small_ps[:, 0, :], in_=x_rows[:], identity=ident_bf[:])
         nc.tensor.transpose(out=small_ps[:, 1, :], in_=gb_rows[:], identity=ident_bf[:])
-
         moments(0)
         inverse_root(0)
         nc.scalar.copy(out=gb[:], in_=small_ps[:, 1, 0:4])
@@ -243,58 +261,68 @@ def tile_edgeupdaterwrapper_v01_pa_s_kernel(tc, p, x_down, ln_edge_g, ln_edge_b,
         moments(2)
         inverse_root(2)
         shift_of(1)
-        normalise(1)
+        normalise_on_scalar(1)
         transposes(1)
         x_i_plane(0)
-        x_i_plane(1)
         moments(3)
         inverse_root(3)
-        shift_of(2)
+        normalise_on_vector(2)
         gain_and_bias_tile(0)
         gain_and_bias_tile(1)
-        normalise(2)
+        x_i_plane(1)
         transposes(2)
-        regroup_w(*MX_SLICES[0])
+        regroup_w(0,256)
+        regroup_w(256,128)
+        quantise_w(0,256)
         shift_of(3)
-        regroup_w(*MX_SLICES[1])
-        quantise_w(*MX_SLICES[0])
-        quantise_w(*MX_SLICES[1])
+        quantise_w(256,128)
         gain_and_bias(1)
-        normalise(3)
-        for q in range(2):
-            group(2 * q)
-            group(2 * q + 1)
-            quantise(2 * q)
-            quantise(2 * q + 1)
-            multiply(2 * q)
-            multiply(2 * q + 1)
-            x_i_plane(q + 2)
-            if q == 0:
-                transposes(3)
-            gain_and_bias(q + 2)
+        normalise_on_scalar(3)
+        group(0)
+        group(1)
+        quantise(0)
+        quantise(1)
+        multiply(0)
+        multiply(1)
+        x_i_plane(2)
+        transposes(3)
+        gain_and_bias(2)
+        group(2)
+        group(3)
+        quantise(2)
+        quantise(3)
+        multiply(2)
+        multiply(3)
+        x_i_plane(3)
+        group_scalar(5)
+        gain_and_bias(3)
         add_bias(0)
         add_bias(1)
         relu_and_store(0)
         relu_and_store(1)
-        group_quarter(2)
+        group(4)
         add_bias(2)
-        quantise_quarter(2)
+        quantise(4)
+        quantise(5)
         multiply(4)
         multiply(5)
-        group_quarter(3)
+        group(6)
+        group(7)
         add_bias(3)
-        quantise_quarter(3)
+        quantise(6)
+        quantise(7)
         multiply(6)
         multiply(7)
         relu_and_store(2)
         relu_and_store(3)
-        def relu_on_vector_and_store(t):
-            nc.vector.tensor_scalar(out=result[:, t, :], in0=result[:, t, :], scalar1=0.0, scalar2=None, op0=ALU.max)
-            nc.sync.dma_start(out=out_rows[:, t, :], in_=result[:, t, :])
-
-        for t in range(4, TILES):
-            add_bias(t)
+        add_bias(4)
+        add_bias(5)
+        add_bias(6)
+        add_bias_columns(7,0,192)
+        add_bias_columns(7,192,384)
+        relu_columns_on_vector(7,0,192)
+        relu_columns_on_vector(7,192,384)
         relu_and_store(4)
         relu_and_store(5)
-        relu_on_vector_and_store(6)
-        relu_on_vector_and_store(7)
+        relu_and_store(6)
+        store(7)

@@ -295,34 +295,34 @@ def tile_edgeupdaterwrapper_v01_pa_s_kernel(tc, p, x_down, ln_edge_g, ln_edge_b,
         multiply(3)
         x_i_plane(3)
         group_scalar(5)
-        gain_and_bias(3)
         add_bias(0)
-        add_bias(1)
         relu_and_store(0)
+        gain_and_bias(3)
+        add_bias(1)
         relu_and_store(1)
+        group_scalar(7)
         group(4)
         add_bias(2)
+        relu_and_store(2)
         quantise(4)
         quantise(5)
         multiply(4)
         multiply(5)
         group(6)
-        group(7)
         add_bias(3)
+        relu_and_store(3)
         quantise(6)
+        add_bias(4)
+        relu_and_store(4)
         quantise(7)
         multiply(6)
         multiply(7)
-        relu_and_store(2)
-        relu_and_store(3)
-        add_bias(4)
         add_bias(5)
+        relu_and_store(5)
         add_bias(6)
+        relu_and_store(6)
         add_bias_columns(7,0,192)
         add_bias_columns(7,192,384)
         relu_columns_on_vector(7,0,192)
         relu_columns_on_vector(7,192,384)
-        relu_and_store(4)
-        relu_and_store(5)
-        relu_and_store(6)
         store(7)

@@ -31,8 +31,8 @@ FLOPS = 2 * EDGES * PACK * P * F_OUT
 
 def tile_edgeupdaterwrapper_v01_pa_s_kernel(tc, p, x_down, ln_edge_g, ln_edge_b, W1, b1, out):
     nc = tc.nc
-    p_rows = p.flatten_outer_dims().rearrange("(t e) f -> e t f", e=P)
-    out_rows = out.flatten_outer_dims().rearrange("(t e) n -> e t n", e=P)
+    p_rows = p.flatten_outer_dims().rearrange("(q r c) f -> r q c f", r=P, c=Q_TILES)
+    out_rows = out.flatten_outer_dims().rearrange("(q r c) n -> r q c n", r=P, c=Q_TILES)
 
     with ExitStack() as ctx:
         ctx.enter_context(tc.manual_schedule())
@@ -79,7 +79,7 @@ def tile_edgeupdaterwrapper_v01_pa_s_kernel(tc, p, x_down, ln_edge_g, ln_edge_b,
             return slice(q * Q_EDGES, (q + 1) * Q_EDGES)
 
         def load_p(q):
-            nc.sync.dma_start(out=p_sb[:, tiles_of(q), :], in_=p_rows[:, tiles_of(q), :])
+            nc.sync.dma_start(out=p_sb[:, tiles_of(q), :], in_=p_rows[:, q, :, :])
 
         def moments(q):
             nc.vector.bn_stats(
@@ -165,14 +165,15 @@ def tile_edgeupdaterwrapper_v01_pa_s_kernel(tc, p, x_down, ln_edge_g, ln_edge_b,
 
         def node_plane(place, nodes):
             nc.scalar.copy(
-                out=planes[:, place, :].rearrange("q (i j) -> q i j", j=NODES), in_=nodes.to_broadcast([P, Q_NODES, NODES])
+                out=planes[:, place, :].rearrange("q (c i j) -> q c i j", c=Q_TILES, i=Q_NODES),
+                in_=nodes.to_broadcast([P, Q_TILES, Q_NODES, P // Q_NODES]),
             )
 
         def x_i_plane(q):
-            node_plane(place_of(q, 0), small_ps[:, 0, q * Q_NODES : (q + 1) * Q_NODES].unsqueeze(2))
+            node_plane(place_of(q, 0), small_ps[:, 0, q * Q_NODES : (q + 1) * Q_NODES].unsqueeze(1).unsqueeze(3))
 
         def x_j_plane():
-            node_plane(place_of(0, 1), small_ps[:, 0, 0:NODES].unsqueeze(1))
+            node_plane(place_of(0, 1), small_ps[:, 0, 0:NODES].rearrange("q (j c) -> q c j", c=Q_TILES).unsqueeze(2))
 
         def tile_edges(t):
             return slice(t * P, (t + 1) * P)
@@ -216,10 +217,10 @@ def tile_edgeupdaterwrapper_v01_pa_s_kernel(tc, p, x_down, ln_edge_g, ln_edge_b,
 
         def relu_and_store(t):
             nc.scalar.activation(out=result[:, t, :], in_=result[:, t, :], func=ACT.Relu)
-            nc.sync.dma_start(out=out_rows[:, t, :], in_=result[:, t, :])
+            nc.sync.dma_start(out=out_rows[:, t // Q_TILES, t % Q_TILES, :], in_=result[:, t, :])
 
         def store(t):
-            nc.sync.dma_start(out=out_rows[:, t, :], in_=result[:, t, :])
+            nc.sync.dma_start(out=out_rows[:, t // Q_TILES, t % Q_TILES, :], in_=result[:, t, :])
 
         def add_bias_columns(t, n0, n1):
             nc.vector.tensor_tensor(out=result[:, t, n0:n1], in0=acc_of[t][:, n0:n1], in1=bias_bc[:, n0:n1], op=ALU.add)
@@ -230,8 +231,8 @@ def tile_edgeupdaterwrapper_v01_pa_s_kernel(tc, p, x_down, ln_edge_g, ln_edge_b,
         load_p(0)
         load_p(1)
         load_p(2)
-        load_p(3)
         nc.sync.dma_start(out=w_raw[:], in_=W1.rearrange("(s q) n -> q s n", q=P))
+        load_p(3)
         nc.scalar.dma_start(out=x_rows[0:NODES, :], in_=x_down.flatten_outer_dims())
         nc.gpsimd.memset(gb_rows[:], 0.0)
         nc.scalar.dma_start(out=gb_rows[0:2, :], in_=ln_edge_g.rearrange("(u f) -> u f", u=2))

@@ -215,9 +215,15 @@ def tile_edgeupdaterwrapper_v01_pa_s_kernel(tc, p, x_down, ln_edge_g, ln_edge_b,
         def add_bias(t):
             nc.vector.tensor_tensor(out=result[:, t, :], in0=acc_of[t][:, 0:F_OUT], in1=bias_bc[:], op=ALU.add)
 
-        def relu_and_store(t):
+        def relu(t):
             nc.scalar.activation(out=result[:, t, :], in_=result[:, t, :], func=ACT.Relu)
-            nc.sync.dma_start(out=out_rows[:, t // Q_TILES, t % Q_TILES, :], in_=result[:, t, :])
+
+        def store_quarter(q):
+            nc.sync.dma_start(out=out_rows[:, q, :, :], in_=result[:, tiles_of(q), :])
+
+        def relu_and_store(t):
+            relu(t)
+            store(t)
 
         def store(t):
             nc.sync.dma_start(out=out_rows[:, t // Q_TILES, t % Q_TILES, :], in_=result[:, t, :])
@@ -243,7 +249,7 @@ def tile_edgeupdaterwrapper_v01_pa_s_kernel(tc, p, x_down, ln_edge_g, ln_edge_b,
         nc.gpsimd.memset(x_rows[64:128, :], 0.0)
         make_identity(nc, ident_bf[:])
         make_identity(nc, ident_f32[:])
-        nc.gpsimd.dma_start(out=bias_bc[:], in_=b1.partition_broadcast(P))
+        nc.sync.dma_start(out=bias_bc[:], in_=b1.partition_broadcast(P))
 
         small_ps = ps_small.tile([P, 2, P], BF16)
         nc.tensor.transpose(out=small_ps[:, 0, :], in_=x_rows[:], identity=ident_bf[:])
@@ -297,10 +303,11 @@ def tile_edgeupdaterwrapper_v01_pa_s_kernel(tc, p, x_down, ln_edge_g, ln_edge_b,
         x_i_plane(3)
         group_scalar(5)
         add_bias(0)
-        relu_and_store(0)
+        relu(0)
         gain_and_bias(3)
         add_bias(1)
-        relu_and_store(1)
+        relu(1)
+        store_quarter(0)
         group_scalar(7)
         group(4)
         add_bias(2)

from contextlib import ExitStack

import concourse.mybir as mybir
from concourse.masks import make_identity

F32 = mybir.dt.float32
BF16 = mybir.dt.bfloat16
U32 = mybir.dt.uint32
U8 = mybir.dt.uint8
FP8X4 = mybir.dt.float8_e4m3fn_x4
ALU = mybir.AluOpType
ACT = mybir.ActivationFunctionType

P = 128
PACK = 4
NODES = 32
EDGES = NODES * NODES
ED = 256
F_OUT = 384
TILES = EDGES // P
QUARTERS = 4
Q_TILES = TILES // QUARTERS
Q_EDGES = Q_TILES * P
Q_NODES = NODES // QUARTERS
EPS = 1e-5
X_J = 5
STEPS = (1, 3, 4, 5)
MX_SLICES = ((0, 256), (256, 128))
FLOPS = 2 * EDGES * PACK * P * F_OUT


def tile_edgeupdaterwrapper_v01_pa_s_kernel(tc, p, x_down, ln_edge_g, ln_edge_b, W1, b1, out):
    nc = tc.nc
    p_rows = p.flatten_outer_dims().rearrange("(q r c) f -> r q c f", r=P, c=Q_TILES)
    out_rows = out.flatten_outer_dims().rearrange("(q r c) n -> r q c n", r=P, c=Q_TILES)

    with ExitStack() as ctx:
        ctx.enter_context(tc.manual_schedule())
        keep = ctx.enter_context(tc.tile_pool(name="keep", bufs=1))
        ps_small = ctx.enter_context(tc.psum_pool(name="ps_small", bufs=1))
        ps_t = ctx.enter_context(tc.psum_pool(name="ps_t", bufs=3))
        ps_acc = ctx.enter_context(tc.psum_pool(name="ps_acc", bufs=4))

        p_sb = keep.tile([P, TILES, ED], BF16)
        x_rows = keep.tile([P, P], BF16)
        gb_rows = keep.tile([P, P], BF16)
        w_raw = keep.tile([P, PACK, F_OUT], BF16)
        bias_bc = keep.tile([P, F_OUT], BF16)
        eps_col = keep.tile([P, 1], F32)
        warm = keep.tile([P, 1], F32)
        ident_bf = keep.tile([P, P], BF16)
        ident_f32 = keep.tile([P, P], F32)
        gb = keep.tile([P, 4], F32)
        planes = keep.tile([P, X_J + 2 * STEPS[-1] + 1, Q_EDGES], BF16)
        w_grouped = keep.tile([P, F_OUT, PACK], BF16, align_bytes=64)
        w_codes = keep.tile([P, F_OUT], U32, align_bytes=64)
        w_scales = keep.tile([P, F_OUT], U8, align_bytes=64)
        stats = keep.tile([P, TILES, 3], F32)
        rstd = keep.tile([P, TILES], F32)
        shift = keep.tile([P, TILES], F32)
        xhat = keep.tile([P, TILES, ED], F32)
        grouped = keep.tile([P, EDGES, PACK], BF16, align_bytes=64)
        z_codes = keep.tile([P, EDGES], U32, align_bytes=64)
        z_scales = keep.tile([P, EDGES], U8, align_bytes=64)
        result = keep.tile([P, TILES, F_OUT], F32)
        xt_of = {}
        acc_of = {}

        def places_of(q):
            return slice(X_J - STEPS[q], X_J + 2 * STEPS[q] + 1, STEPS[q])

        def place_of(q, s):
            return X_J + (s - 1) * STEPS[q]

        def tiles_of(q):
            return slice(q * Q_TILES, (q + 1) * Q_TILES)

        def edges_of(q):
            return slice(q * Q_EDGES, (q + 1) * Q_EDGES)

        def load_p(q):
            nc.sync.dma_start(out=p_sb[:, tiles_of(q), :], in_=p_rows[:, q, :, :])

        def moments(q):
            nc.vector.bn_stats(
                out=stats[:, tiles_of(q), :].rearrange("e t c -> e (t c)"),
                in_=p_sb[:, tiles_of(q), :].rearrange("e t f -> e f t"),
            )

        def inverse_root(q):
            nc.scalar.activation(
                out=rstd[:, tiles_of(q)], in_=stats[:, tiles_of(q), 2], func=ACT.Abs_reciprocal_sqrt,
                bias=eps_col[:], scale=1.0 / ED,
            )

        def shift_of(q):
            nc.vector.scalar_tensor_tensor(
                out=shift[:, tiles_of(q)], in0=stats[:, tiles_of(q), 1], scalar=-1.0, in1=rstd[:, tiles_of(q)],
                op0=ALU.mult, op1=ALU.mult,
            )

        def normalise_tile(t):
            nc.scalar.activation(
                out=xhat[:, t, :], in_=p_sb[:, t, :], func=ACT.Identity,
                scale=rstd[:, t : t + 1], bias=shift[:, t : t + 1],
            )

        def normalise_on_scalar(q):
            for t in (2 * q, 2 * q + 1):
                normalise_tile(t)

        def normalise_on_vector(q):
            for t in (2 * q, 2 * q + 1):
                nc.vector.tensor_scalar(
                    out=xhat[:, t, :], in0=p_sb[:, t, :], scalar1=stats[:, t, 1:2], scalar2=rstd[:, t : t + 1],
                    op0=ALU.subtract, op1=ALU.mult,
                )

        def transpose_tile(t):
            q, c = divmod(t, Q_TILES)
            if c == 0:
                xt_of[q] = ps_t.tile([P, 2, Q_EDGES], F32, name="xt")
            for u in range(2):
                nc.tensor.transpose(
                    out=xt_of[q][:, u, c * P : (c + 1) * P], in_=xhat[:, t, u * P : (u + 1) * P], identity=ident_f32[:]
                )

        def transposes(q):
            transpose_tile(2 * q)
            transpose_tile(2 * q + 1)

        def gain_and_bias(q):
            for u in range(2):
                nc.scalar.activation(
                    out=planes[:, place_of(q, 2 + u), :], in_=xt_of[q][:, u, :], func=ACT.Identity,
                    scale=gb[:, u : u + 1], bias=gb[:, 2 + u : 3 + u],
                )

        def gain_and_bias_tile(t):
            q, c = divmod(t, Q_TILES)
            for u in range(2):
                nc.scalar.activation(
                    out=planes[:, place_of(q, 2 + u), c * P : (c + 1) * P], in_=xt_of[q][:, u, c * P : (c + 1) * P], func=ACT.Identity,
                    scale=gb[:, u : u + 1], bias=gb[:, 2 + u : 3 + u],
                )

        def regroup_w(n0, nw):
            nc.vector.tensor_copy(
                out=w_grouped[:, n0 : n0 + nw, :].rearrange("q (c i) s -> q c s i", i=4),
                in_=w_raw[:, :, n0 : n0 + nw].rearrange("q s (c i) -> q c s i", i=4),
            )

        def regroup_w_scalar(n0, nw):
            nc.scalar.copy(
                out=w_grouped[:, n0 : n0 + nw, :].rearrange("q (c i) s -> q c s i", i=4),
                in_=w_raw[:, :, n0 : n0 + nw].rearrange("q s (c i) -> q c s i", i=4),
            )

        def quantise_w(n0, nw):
            nc.vector.quantize_mx(
                out=w_codes[:, n0 : n0 + nw].bitcast(FP8X4),
                scales=w_scales[:, n0 : n0 + nw],
                in_=w_grouped[:, n0 : n0 + nw, :].rearrange("q n s -> q (n s)"),
            )

        def node_plane(place, nodes):
            nc.scalar.copy(
                out=planes[:, place, :].rearrange("q (c i j) -> q c i j", c=Q_TILES, i=Q_NODES),
                in_=nodes.to_broadcast([P, Q_TILES, Q_NODES, P // Q_NODES]),
            )

        def x_i_plane(q):
            node_plane(place_of(q, 0), small_ps[:, 0, q * Q_NODES : (q + 1) * Q_NODES].unsqueeze(1).unsqueeze(3))

        def x_j_plane():
            node_plane(place_of(0, 1), small_ps[:, 0, 0:NODES].rearrange("q (j c) -> q c j", c=Q_TILES).unsqueeze(2))

        def tile_edges(t):
            return slice(t * P, (t + 1) * P)

        def group(t):
            nc.vector.tensor_copy(
                out=grouped[:, tile_edges(t), :].rearrange("q (c i) s -> q c s i", i=4),
                in_=planes[:, places_of(t // 2), (t % 2) * P : (t % 2 + 1) * P].rearrange("q s (c i) -> q c s i", i=4),
            )

        def group_scalar(t):
            nc.scalar.copy(
                out=grouped[:, tile_edges(t), :].rearrange("q (c i) s -> q c s i", i=4),
                in_=planes[:, places_of(t // 2), (t % 2) * P : (t % 2 + 1) * P].rearrange("q s (c i) -> q c s i", i=4),
            )

        def quantise(t):
            nc.vector.quantize_mx(
                out=z_codes[:, tile_edges(t)].bitcast(FP8X4),
                scales=z_scales[:, tile_edges(t)],
                in_=grouped[:, tile_edges(t), :].rearrange("q e s -> q (e s)"),
            )

        def multiply(t):
            acc = ps_acc.tile([P, 512], F32, name="acc")
            acc_of[t] = acc
            es = slice(t * P, (t + 1) * P)
            for n0, nw in MX_SLICES:
                nc.tensor.matmul_mx(
                    out=acc[:, n0 : n0 + nw],
                    lhsT=z_codes[:, es].bitcast(FP8X4),
                    lhsT_scale=z_scales[:, es],
                    rhs=w_codes[:, n0 : n0 + nw].bitcast(FP8X4),
                    rhs_scale=w_scales[:, n0 : n0 + nw],
                    start=True,
                    stop=True,
                )

        def add_bias(t):
            nc.vector.tensor_tensor(out=result[:, t, :], in0=acc_of[t][:, 0:F_OUT], in1=bias_bc[:], op=ALU.add)

        def relu(t):
            nc.scalar.activation(out=result[:, t, :], in_=result[:, t, :], func=ACT.Relu)

        def store_quarter(q):
            nc.sync.dma_start(out=out_rows[:, q, :, :], in_=result[:, tiles_of(q), :])

        def relu_and_store(t):
            relu(t)
            store(t)

        def store(t):
            nc.sync.dma_start(out=out_rows[:, t // Q_TILES, t % Q_TILES, :], in_=result[:, t, :])

        def add_bias_columns(t, n0, n1):
            nc.vector.tensor_tensor(out=result[:, t, n0:n1], in0=acc_of[t][:, n0:n1], in1=bias_bc[:, n0:n1], op=ALU.add)

        def relu_columns_on_vector(t, n0, n1):
            nc.vector.tensor_scalar(out=result[:, t, n0:n1], in0=result[:, t, n0:n1], scalar1=0.0, scalar2=None, op0=ALU.max)

        load_p(0)
        load_p(1)
        load_p(2)
        nc.sync.dma_start(out=w_raw[:], in_=W1.rearrange("(s q) n -> q s n", q=P))
        load_p(3)
        nc.scalar.dma_start(out=x_rows[0:NODES, :], in_=x_down.flatten_outer_dims())
        nc.gpsimd.memset(gb_rows[:], 0.0)
        nc.scalar.dma_start(out=gb_rows[0:2, :], in_=ln_edge_g.rearrange("(u f) -> u f", u=2))
        nc.scalar.dma_start(out=gb_rows[2:4, :], in_=ln_edge_b.rearrange("(u f) -> u f", u=2))
        nc.gpsimd.memset(eps_col[:], EPS)
        nc.scalar.activation(out=warm[:], in_=eps_col[:], func=ACT.Abs_reciprocal_sqrt)
        nc.gpsimd.memset(x_rows[32:64, :], 0.0)
        nc.gpsimd.memset(x_rows[64:128, :], 0.0)
        make_identity(nc, ident_bf[:])
        make_identity(nc, ident_f32[:])
        nc.sync.dma_start(out=bias_bc[:], in_=b1.partition_broadcast(P))

        small_ps = ps_small.tile([P, 2, P], BF16)
        nc.tensor.transpose(out=small_ps[:, 0, :], in_=x_rows[:], identity=ident_bf[:])
        nc.tensor.transpose(out=small_ps[:, 1, :], in_=gb_rows[:], identity=ident_bf[:])
        moments(0)
        inverse_root(0)
        nc.scalar.copy(out=gb[:], in_=small_ps[:, 1, 0:4])
        x_j_plane()
        moments(1)
        inverse_root(1)
        shift_of(0)
        normalise_tile(0)
        transpose_tile(0)
        normalise_tile(1)
        transpose_tile(1)
        moments(2)
        inverse_root(2)
        shift_of(1)
        normalise_on_scalar(1)
        transposes(1)
        x_i_plane(0)
        moments(3)
        inverse_root(3)
        normalise_on_vector(2)
        gain_and_bias_tile(0)
        gain_and_bias_tile(1)
        x_i_plane(1)
        transposes(2)
        regroup_w(0,256)
        regroup_w(256,128)
        quantise_w(0,256)
        shift_of(3)
        quantise_w(256,128)
        gain_and_bias(1)
        normalise_on_scalar(3)
        group(0)
        group(1)
        quantise(0)
        quantise(1)
        multiply(0)
        multiply(1)
        x_i_plane(2)
        transposes(3)
        gain_and_bias(2)
        group(2)
        group(3)
        quantise(2)
        quantise(3)
        multiply(2)
        multiply(3)
        x_i_plane(3)
        group_scalar(5)
        add_bias(0)
        relu(0)
        gain_and_bias(3)
        add_bias(1)
        relu(1)
        store_quarter(0)
        group_scalar(7)
        group(4)
        add_bias(2)
        relu_and_store(2)
        quantise(4)
        quantise(5)
        multiply(4)
        multiply(5)
        group(6)
        add_bias(3)
        relu_and_store(3)
        quantise(6)
        add_bias(4)
        relu_and_store(4)
        quantise(7)
        multiply(6)
        multiply(7)
        add_bias(5)
        relu_and_store(5)
        add_bias(6)
        relu_and_store(6)
        add_bias_columns(7,0,192)
        add_bias_columns(7,192,384)
        relu_columns_on_vector(7,0,192)
        relu_columns_on_vector(7,192,384)
        store(7)
